import numpy as np
import ml_dtypes


def mxq(x, axis, fmt="e4m3"):
    dtype, down = {"e4m3": (ml_dtypes.float8_e4m3fn, 7), "e5m2": (ml_dtypes.float8_e5m2, 14)}[fmt]
    v = np.moveaxis(np.asarray(x, np.float32).astype(ml_dtypes.bfloat16).astype(np.float64), axis, -1)
    blocks = v.reshape(v.shape[:-1] + (-1, 32))
    amax = np.abs(blocks).max(-1, keepdims=True)
    byte = np.maximum(np.where(amax > 0, np.frexp(amax)[1] - 1 + 127, 0) - down, 1)
    scale = np.exp2(byte - 127.0)
    codes = (blocks / scale).astype(np.float32).astype(dtype).astype(np.float64)
    return np.moveaxis((codes * scale).reshape(v.shape), -1, axis)


WIDE = False


def mx_kscale(k):
    if not WIDE:
        return np.ones(k)
    levels = np.array([10, -10, 5, -5, 0])
    a = np.random.permutation(np.resize(levels, k // 512 * 4)).reshape(k // 512, 4)
    idx = np.arange(k)
    return np.exp2(a[idx // 512, idx % 128 // 32])


BF16 = ml_dtypes.bfloat16


def bf(x):
    return np.asarray(x, np.float32).astype(BF16)


def f64(x):
    return np.asarray(x).astype(np.float64)


E2M1 = np.array([0.0, 0.5, 1.0, 1.5, 2.0, 3.0, 4.0, 6.0, -0.0, -0.5, -1.0, -1.5, -2.0, -3.0, -4.0, -6.0])


def pack_weight(w, fmt):
    k, n = w.shape
    w = f64(bf(w)).reshape(k // 32, 32, n)
    amax = np.abs(w).max(1)
    if fmt == "e4m3":
        byte = np.frexp(amax)[1] - 1 + 127 - 7
    else:
        mant, ex = np.frexp(amax / 6.0)
        byte = np.where(mant > 0.5, ex, ex - 1) + 127
    byte = np.clip(np.where(amax > 0, byte, 1), 1, 254)
    scaled = (w * np.exp2(127.0 - byte)[:, None, :]).reshape(k, n).astype(np.float32)
    by_word = np.ascontiguousarray(scaled.reshape(k // 512, 128, 4, n).transpose(0, 1, 3, 2))
    if fmt == "e4m3":
        words = by_word.astype(ml_dtypes.float8_e4m3fn).view(np.uint8)
    else:
        c = by_word.astype(ml_dtypes.float4_e2m1fn).view(np.uint8) & 0xF
        words = c[..., 0::2] | (c[..., 1::2] << 4)
    return np.ascontiguousarray(words), np.ascontiguousarray(byte.astype(np.uint8).reshape(k // 512, 16, n))


def unpack_weight(words, scales, fmt):
    g, p, n, _ = words.shape
    if fmt == "e4m3":
        vals = np.ascontiguousarray(words).view(ml_dtypes.float8_e4m3fn).astype(np.float64)
    else:
        nib = np.empty((g, p, n, 4), np.uint8)
        nib[..., 0::2] = words & 0xF
        nib[..., 1::2] = words >> 4
        vals = E2M1[nib]
    vals = vals * np.repeat(np.exp2(scales.astype(np.float64) - 127.0), 8, axis=1)[..., None]
    return vals.transpose(0, 1, 3, 2).reshape(g * 512, n)

def pack4(w):
    words, scales = pack_weight(w, "e2m1")
    return words.reshape(words.shape[0], 128, -1), scales


def unpack4(words, scales):
    return unpack_weight(words.reshape(words.shape[0], 128, -1, 2), scales, "e2m1")


B, In, H, Hh, E, G = 512, 1024, 1024, 256, 128, 4
K = In + H
EPS = 1e-6


def rn(*shape):
    return np.random.standard_normal(shape)


def sigmoid(v):
    return 1.0 / (1.0 + np.exp(-v))


def ln(a, gamma, beta):
    mean = a.mean(-1, keepdims=True)
    std = a.std(-1, keepdims=True, ddof=1)
    return gamma * (a - mean) / (std + EPS) + beta


def setup_inputs():
    s = mx_kscale(K)
    x = bf(rn(B, In) * s[:In])
    h = bf(rn(B, H) * s[In:])
    hyper_h = bf(rn(B, Hh))
    hyper_c = bf(rn(B, Hh))
    wih = rn(G * Hh, K) / np.sqrt(K) / s[None, :]
    hc_Wih_words, hc_Wih_scales = pack4(np.ascontiguousarray(wih.T))
    return {
        'x': x,
        'h': h,
        'hyper_h': hyper_h,
        'hyper_c': hyper_c,
        'hc_Wih_words': hc_Wih_words,
        'hc_Wih_scales': hc_Wih_scales,
        'hc_bih': bf(0.3 * rn(G * Hh)),
        'hc_Whh': bf(rn(G * Hh, Hh) / np.sqrt(Hh)),
        'hc_ln_gamma': bf(1.0 + 0.1 * rn(G, Hh)),
        'hc_ln_beta': bf(0.1 * rn(G, Hh)),
        'hc_lnc_gamma': bf(1.0 + 0.1 * rn(Hh)),
        'hc_lnc_beta': bf(0.1 * rn(Hh)),
    }


def reference(x, h, hyper_h, hyper_c, hc_Wih_words, hc_Wih_scales, hc_bih, hc_Whh, hc_ln_gamma, hc_ln_beta, hc_lnc_gamma, hc_lnc_beta):
    hyper_in = np.concatenate([f64(x), f64(h)], axis=1)
    v = (mxq(hyper_in, 1, 'e4m3') @ unpack4(hc_Wih_words, hc_Wih_scales)) + f64(hc_bih) + f64(hyper_h) @ f64(hc_Whh).T
    v = ln(v.reshape(B, G, Hh), f64(hc_ln_gamma), f64(hc_ln_beta))
    hi, hf, hg, ho = v[:, 0], v[:, 1], v[:, 2], v[:, 3]
    hf = hf + 1.0
    new_hyper_c = f64(hyper_c) * sigmoid(hf) + sigmoid(hi) * np.tanh(hg)
    new_hyper_c = ln(new_hyper_c, f64(hc_lnc_gamma), f64(hc_lnc_beta))
    new_hyper_h = np.tanh(new_hyper_c) * sigmoid(ho)
    return new_hyper_h, new_hyper_c

@@ -1,0 +1,332 @@
+from contextlib import ExitStack
+import math
+
+import concourse.mybir as mybir
+from concourse.masks import make_identity
+
+F32 = mybir.dt.float32
+BF16 = mybir.dt.bfloat16
+I32 = mybir.dt.int32
+U32 = mybir.dt.uint32
+U8 = mybir.dt.uint8
+FP8X4 = mybir.dt.float8_e4m3fn_x4
+FP4X4 = mybir.dt.float4_e2m1fn_x4
+ALU = mybir.AluOpType
+ACT = mybir.ActivationFunctionType
+
+P = 128
+BATCH, IN, HID, UNITS, GATES = 512, 1024, 1024, 256, 4
+K = IN + HID
+N = GATES * UNITS
+K_PASS = 4 * P
+PASSES = K // K_PASS
+BANK = 512
+HALVES = N // BANK
+GATES_PER_BANK = BANK // UNITS
+BATCH_TILES = BATCH // P
+K_PLAIN = UNITS // P
+EPS = 1e-6
+ROOT_TO_STD = 1.0 / (UNITS * math.sqrt(UNITS - 1))
+
+FLOPS = 2 * BATCH * K * N + 2 * BATCH * UNITS * N
+
+
+def gate_cols(j):
+    return slice(j * UNITS, (j + 1) * UNITS)
+
+
+def tile_hyperlstmcell_pa_kernel(
+    tc,
+    x,
+    h,
+    hyper_h,
+    hyper_c,
+    hc_Wih_words,
+    hc_Wih_scales,
+    hc_bih,
+    hc_Whh,
+    hc_ln_gamma,
+    hc_ln_beta,
+    hc_lnc_gamma,
+    hc_lnc_beta,
+    out_0,
+    out_1,
+):
+    nc = tc.nc
+    with ExitStack() as ctx:
+        keep = ctx.enter_context(tc.tile_pool(name="keep", bufs=1))
+        stage = ctx.enter_context(tc.tile_pool(name="stage", bufs=2))
+        post = ctx.enter_context(tc.tile_pool(name="post", bufs=2))
+        stats = ctx.enter_context(tc.tile_pool(name="stats", bufs=2))
+        const_psum = ctx.enter_context(tc.psum_pool(name="const_psum", bufs=1))
+        work_psum = ctx.enter_context(tc.psum_pool(name="work_psum", bufs=3))
+        mx_psum = ctx.enter_context(tc.psum_pool(name="mx_psum", bufs=2))
+        ctx.enter_context(tc.manual_schedule())
+
+        ident_f32 = keep.tile([P, P], F32)
+        make_identity(nc, ident_f32[:])
+        ident_bf16 = keep.tile([P, P], BF16)
+        make_identity(nc, ident_bf16[:])
+        norm_rows = keep.tile([P, P], BF16)
+        nc.vector.memset(norm_rows[:], 0.0)
+        bias_row = keep.tile([P, N], BF16)
+        nc.vector.memset(bias_row[:], 0.0)
+        w_scales = keep.tile([P, PASSES, N], U8, align_bytes=64)
+        nc.vector.memset(w_scales[:].bitcast(I32), 0)
+        gate_shift = keep.tile([P, GATES], F32)
+        nc.vector.memset(gate_shift[:], 0.0)
+        nc.vector.memset(gate_shift[:, 1:2], 1.0)
+        ones = keep.tile([P, P], BF16)
+        nc.vector.memset(ones[:], 1.0)
+        half = keep.tile([P, GATES], F32)
+        nc.vector.memset(half[:], 0.5)
+
+        nc.scalar.dma_start(out=norm_rows[0:8, :], in_=hc_ln_gamma.rearrange("g (c n) -> (g c) n", n=P))
+        nc.scalar.dma_start(out=norm_rows[8:16, :], in_=hc_ln_beta.rearrange("g (c n) -> (g c) n", n=P))
+        nc.scalar.dma_start(out=norm_rows[16:18, :], in_=hc_lnc_gamma.rearrange("(c n) -> c n", n=P))
+        nc.scalar.dma_start(out=norm_rows[18:20, :], in_=hc_lnc_beta.rearrange("(c n) -> c n", n=P))
+        nc.scalar.dma_start(out=bias_row[0:1, :], in_=hc_bih.unsqueeze(0))
+        warm = keep.tile([P, 1], F32)
+        nc.scalar.activation(out=warm[:], in_=gate_shift[:, 0:1], func=ACT.Sigmoid)
+
+        hh_sb = [keep.tile([P, UNITS], BF16, name="hh_sb%d" % t) for t in range(BATCH_TILES)]
+        hc_sb = [keep.tile([P, UNITS], BF16, name="hc_sb%d" % t) for t in range(BATCH_TILES)]
+        u_sb = [keep.tile([P, K], BF16, name="u_sb%d" % t) for t in range(BATCH_TILES)]
+
+        def load_rows(t):
+            rows = slice(t * P, (t + 1) * P)
+            nc.sync.dma_start(out=hh_sb[t][:], in_=hyper_h[rows, :])
+            nc.sync.dma_start(out=u_sb[t][:, 0:IN], in_=x[rows, :])
+            nc.sync.dma_start(out=u_sb[t][:, IN:K], in_=h[rows, :])
+            nc.sync.dma_start(out=hc_sb[t][:], in_=hyper_c[rows, :])
+
+        load_rows(0)
+        whh_sb = keep.tile([P, N // P, UNITS], BF16)
+        nc.sync.dma_start(out=whh_sb[:], in_=hc_Whh.rearrange("(c p) k -> p c k", p=P))
+        w_words = keep.tile([P, PASSES, 2 * N], U8, align_bytes=64)
+        for g in range(PASSES):
+            nc.sync.dma_start(out=w_words[:, g, :].bitcast(I32), in_=hc_Wih_words[g].bitcast(I32))
+        for quad in range(4):
+            nc.sync.dma_start(
+                out=w_scales[32 * quad : 32 * quad + 4, :, :].bitcast(I32),
+                in_=hc_Wih_scales[:, 4 * quad : 4 * quad + 4, :].bitcast(I32).rearrange("g r c -> r g c"),
+            )
+        for t in range(1, BATCH_TILES):
+            load_rows(t)
+
+        hhT = [keep.tile([P, K_PLAIN, P], BF16, name="hhT%d" % t) for t in range(BATCH_TILES)]
+        u_codes = [keep.tile([P, PASSES * P], U32, name="u_codes%d" % t, align_bytes=64) for t in range(BATCH_TILES)]
+        u_scales = [keep.tile([P, PASSES * P], U8, name="u_scales%d" % t, align_bytes=64) for t in range(BATCH_TILES)]
+        plain = [keep.tile([P, N], F32, name="plain%d" % t) for t in range(BATCH_TILES)]
+        whhT = keep.tile([P, K_PLAIN, N], BF16)
+        gamma_bc = const_psum.tile([P, N], BF16)
+        beta_bc = const_psum.tile([P, N], BF16)
+        c_norm_bc = const_psum.tile([P, 2 * UNITS], BF16)
+
+        def transpose_rows(t):
+            hh_bank = work_psum.tile([P, K_PLAIN, P], BF16, tag="work")
+            for kk in range(K_PLAIN):
+                nc.tensor.transpose(hh_bank[:, kk, :], hh_sb[t][:, kk * P : (kk + 1) * P], ident_bf16[:])
+            nc.scalar.copy(out=hhT[t][:], in_=hh_bank[:])
+            u_words = u_sb[t][:].bitcast(F32)
+            grouped = stage.tile([P, PASSES, P, 4], BF16, align_bytes=64)
+            grouped_words = grouped[:].bitcast(F32)
+            for pair in range(PASSES // 2):
+                planes = work_psum.tile([P, 2, 2, P], F32, tag="work")
+                for gg in range(2):
+                    g = 2 * pair + gg
+                    for w in range(2):
+                        nc.tensor.transpose(
+                            planes[:, gg, w, :], u_words[:, 256 * g + w : 256 * (g + 1) : 2], ident_f32[:]
+                        )
+                nc.scalar.copy(
+                    out=grouped_words[:, 2 * pair : 2 * pair + 2, :, :],
+                    in_=planes[:].rearrange("p g w b -> p g b w"),
+                )
+            return grouped
+
+        def quantise(t, grouped):
+            nc.vector.quantize_mx(
+                out=u_codes[t][:].bitcast(FP8X4),
+                scales=u_scales[t][:],
+                in_=grouped[:].rearrange("p g b j -> p (g b j)"),
+            )
+
+        def plain_product(t):
+            for half_n in range(HALVES):
+                cols = slice(half_n * BANK, (half_n + 1) * BANK)
+                acc = work_psum.tile([P, BANK], F32, tag="work")
+                for kk in range(K_PLAIN):
+                    nc.tensor.matmul(acc[:], lhsT=hhT[t][:, kk, :], rhs=whhT[:, kk, cols], start=(kk == 0), stop=False)
+                nc.tensor.matmul(acc[:], lhsT=ones[:], rhs=bias_row[:, cols], start=False, stop=True)
+                nc.scalar.copy(out=plain[t][:, cols], in_=acc[:])
+
+        def mx_product(t):
+            banks = []
+            for half_n in range(HALVES):
+                acc = mx_psum.tile([P, BANK], F32, tag="mx", name="mx_acc")
+                for g in range(PASSES):
+                    rows = slice(g * P, (g + 1) * P)
+                    nc.tensor.matmul_mx(
+                        out=acc[:],
+                        lhsT=u_codes[t][:, rows].bitcast(FP8X4),
+                        lhsT_scale=u_scales[t][:, rows],
+                        rhs=w_words[:, g, 2 * half_n * BANK : 2 * (half_n + 1) * BANK].bitcast(FP4X4),
+                        rhs_scale=w_scales[:, g, half_n * BANK : (half_n + 1) * BANK],
+                        start=(g == 0),
+                        stop=(g == PASSES - 1),
+                    )
+                banks.append(acc)
+            return banks
+
+        def std_plus_eps(scaled_sq, width, tag):
+            root = stats.tile([P, width], F32, tag=tag + "_root")
+            nc.gpsimd.tensor_tensor(out=root[:], in0=scaled_sq[:], in1=half[:, 0:width], op=ALU.pow)
+            std = stats.tile([P, width], F32, tag=tag + "_std")
+            nc.gpsimd.tensor_scalar(
+                out=std[:], in0=root[:], scalar1=ROOT_TO_STD, scalar2=EPS, op0=ALU.mult, op1=ALU.add
+            )
+            return std
+
+        def join_and_centre(t, banks):
+            v = post.tile([P, N], F32, tag="v")
+            sums = stats.tile([P, GATES], F32, tag="sums")
+            scaled_sq = stats.tile([P, GATES], F32, tag="scaled_sq")
+            for j in range(GATES):
+                in_bank = gate_cols(j % GATES_PER_BANK)
+                nc.vector.scalar_tensor_tensor(
+                    out=v[:, gate_cols(j)],
+                    in0=banks[j // GATES_PER_BANK][:, in_bank],
+                    scalar=1.0,
+                    in1=plain[t][:, gate_cols(j)],
+                    op0=ALU.mult,
+                    op1=ALU.add,
+                    accum_out=sums[:, j : j + 1],
+                )
+                squares = post.tile([P, UNITS], F32, tag="squares")
+                nc.scalar.activation(
+                    out=squares[:],
+                    in_=v[:, gate_cols(j)],
+                    func=ACT.Square,
+                    scale=-float(UNITS),
+                    bias=sums[:, j : j + 1],
+                    accum_out=scaled_sq[:, j : j + 1],
+                )
+            std = std_plus_eps(scaled_sq, GATES, "gate")
+            neg_mean = stats.tile([P, GATES], F32, tag="neg_mean")
+            nc.vector.tensor_scalar_mul(out=neg_mean[:], in0=sums[:], scalar1=-1.0 / UNITS)
+            centred = post.tile([P, N], F32, tag="centred")
+            for j in range(GATES):
+                nc.vector.scalar_tensor_tensor(
+                    out=centred[:, gate_cols(j)],
+                    in0=v[:, gate_cols(j)],
+                    scalar=neg_mean[:, j : j + 1],
+                    in1=gamma_bc[:, gate_cols(j)],
+                    op0=ALU.add,
+                    op1=ALU.mult,
+                )
+            return centred, std
+
+        def activate(centred, std):
+            inv = stats.tile([P, GATES], F32, tag="inv")
+            nc.vector.reciprocal(out=inv[:], in_=std[:])
+            normed = post.tile([P, N], F32, tag="normed")
+            act = post.tile([P, N], F32, tag="act")
+            for j, func in enumerate((ACT.Sigmoid, ACT.Sigmoid, ACT.Tanh, ACT.Sigmoid)):
+                nc.vector.scalar_tensor_tensor(
+                    out=normed[:, gate_cols(j)],
+                    in0=centred[:, gate_cols(j)],
+                    scalar=inv[:, j : j + 1],
+                    in1=beta_bc[:, gate_cols(j)],
+                    op0=ALU.mult,
+                    op1=ALU.add,
+                )
+                nc.scalar.activation(
+                    out=act[:, gate_cols(j)], in_=normed[:, gate_cols(j)], func=func, bias=gate_shift[:, j : j + 1]
+                )
+            return act
+
+        def cell_sum(t, act):
+            kept = post.tile([P, UNITS], F32, tag="kept")
+            nc.vector.tensor_tensor(out=kept[:], in0=hc_sb[t][:], in1=act[:, gate_cols(1)], op=ALU.mult)
+            written = post.tile([P, UNITS], F32, tag="written")
+            nc.vector.tensor_tensor(out=written[:], in0=act[:, gate_cols(0)], in1=act[:, gate_cols(2)], op=ALU.mult)
+            raw_c = post.tile([P, UNITS], F32, tag="raw_c")
+            c_sum = stats.tile([P, 1], F32, tag="c_sum")
+            nc.vector.scalar_tensor_tensor(
+                out=raw_c[:], in0=kept[:], scalar=1.0, in1=written[:], op0=ALU.mult, op1=ALU.add, accum_out=c_sum[:]
+            )
+            c_scaled_sq = stats.tile([P, 1], F32, tag="c_scaled_sq")
+            c_squares = post.tile([P, UNITS], F32, tag="squares")
+            nc.scalar.activation(
+                out=c_squares[:],
+                in_=raw_c[:],
+                func=ACT.Square,
+                scale=-float(UNITS),
+                bias=c_sum[:],
+                accum_out=c_scaled_sq[:],
+            )
+            c_std = std_plus_eps(c_scaled_sq, 1, "cell")
+            c_neg_mean = stats.tile([P, 1], F32, tag="c_neg_mean")
+            nc.vector.tensor_scalar_mul(out=c_neg_mean[:], in0=c_sum[:], scalar1=-1.0 / UNITS)
+            c_centred = post.tile([P, UNITS], F32, tag="c_centred")
+            nc.vector.scalar_tensor_tensor(
+                out=c_centred[:], in0=raw_c[:], scalar=c_neg_mean[:], in1=c_norm_bc[:, 0:UNITS], op0=ALU.add, op1=ALU.mult
+            )
+            return c_centred, c_std
+
+        def cell_finish(t, c_centred, c_std, act):
+            rows = slice(t * P, (t + 1) * P)
+            c_inv = stats.tile([P, 1], F32, tag="c_inv")
+            nc.vector.reciprocal(out=c_inv[:], in_=c_std[:])
+            new_c = post.tile([P, UNITS], F32, tag="new_c")
+            nc.vector.scalar_tensor_tensor(
+                out=new_c[:], in0=c_centred[:], scalar=c_inv[:], in1=c_norm_bc[:, UNITS : 2 * UNITS], op0=ALU.mult, op1=ALU.add
+            )
+            nc.sync.dma_start(out=out_1[rows, :], in_=new_c[:])
+            tanh_c = post.tile([P, UNITS], F32, tag="tanh_c")
+            nc.scalar.activation(out=tanh_c[:], in_=new_c[:], func=ACT.Tanh)
+            new_h = post.tile([P, UNITS], F32, tag="new_h")
+            nc.vector.tensor_tensor(out=new_h[:], in0=tanh_c[:], in1=act[:, gate_cols(3)], op=ALU.mult)
+            nc.sync.dma_start(out=out_0[rows, :], in_=new_h[:])
+
+        norm_cols_bank = work_psum.tile([P, P], BF16, tag="work")
+        nc.tensor.transpose(norm_cols_bank[:], norm_rows[:], ident_bf16[:])
+        norm_cols = keep.tile([P, 20], BF16)
+        nc.vector.tensor_copy(out=norm_cols[:], in_=norm_cols_bank[:, 0:20])
+        grouped = transpose_rows(0)
+        quantise(0, grouped)
+        for kk in range(K_PLAIN):
+            whh_bank = work_psum.tile([P, N], BF16, tag="work")
+            for c in range(N // P):
+                nc.tensor.transpose(
+                    whh_bank[:, c * P : (c + 1) * P], whh_sb[:, c, kk * P : (kk + 1) * P], ident_bf16[:]
+                )
+            nc.vector.tensor_copy(out=whhT[:, kk, :], in_=whh_bank[:])
+        for first, spread in ((0, gamma_bc), (8, beta_bc), (16, c_norm_bc)):
+            for c in range(spread.shape[1] // P):
+                nc.tensor.transpose(
+                    spread[:, c * P : (c + 1) * P],
+                    norm_cols[:, first + c : first + c + 1].to_broadcast([P, P]),
+                    ident_bf16[:],
+                )
+        plain_product(0)
+        banks = mx_product(0)
+
+        act = None
+        for t in range(BATCH_TILES + 1):
+            if t + 1 < BATCH_TILES:
+                grouped = transpose_rows(t + 1)
+            if t < BATCH_TILES:
+                centred, std = join_and_centre(t, banks)
+            if t + 1 < BATCH_TILES:
+                quantise(t + 1, grouped)
+                plain_product(t + 1)
+                banks = mx_product(t + 1)
+            if t >= 1:
+                c_centred, c_std = cell_sum(t - 1, act)
+            older_act = act
+            if t < BATCH_TILES:
+                act = activate(centred, std)
+            if t >= 1:
+                cell_finish(t - 1, c_centred, c_std, older_act)

@@ -27,12 +27,23 @@ BATCH_TILES = BATCH // P
 K_PLAIN = UNITS // P
 EPS = 1e-6
 ROOT_TO_STD = 1.0 / (UNITS * math.sqrt(UNITS - 1))
+GATE_I, GATE_F, GATE_G, GATE_O = 0, 1, 2, 3
+CELL_GATES = (GATE_I, GATE_F, GATE_G)
+GATE_FUNC = (ACT.Sigmoid, ACT.Sigmoid, ACT.Tanh, ACT.Sigmoid)
 
 FLOPS = 2 * BATCH * K * N + 2 * BATCH * UNITS * N
 
 
 def gate_cols(j):
     return slice(j * UNITS, (j + 1) * UNITS)
+
+
+def batch_rows(t):
+    return slice(t * P, (t + 1) * P)
+
+
+def live(t):
+    return 0 <= t < BATCH_TILES
 
 
 def tile_hyperlstmcell_pa_kernel(
@@ -55,13 +66,16 @@ def tile_hyperlstmcell_pa_kernel(
     nc = tc.nc
     with ExitStack() as ctx:
         keep = ctx.enter_context(tc.tile_pool(name="keep", bufs=1))
-        stage = ctx.enter_context(tc.tile_pool(name="stage", bufs=2))
-        post = ctx.enter_context(tc.tile_pool(name="post", bufs=2))
-        stats = ctx.enter_context(tc.tile_pool(name="stats", bufs=2))
+        scrap = ctx.enter_context(tc.tile_pool(name="scrap", bufs=2))
         const_psum = ctx.enter_context(tc.psum_pool(name="const_psum", bufs=1))
         work_psum = ctx.enter_context(tc.psum_pool(name="work_psum", bufs=3))
         mx_psum = ctx.enter_context(tc.psum_pool(name="mx_psum", bufs=2))
         ctx.enter_context(tc.manual_schedule())
+
+        def per_tile(name, shape, dtype, align_bytes=32):
+            return [
+                keep.tile(shape, dtype, name="%s%d" % (name, t), align_bytes=align_bytes) for t in range(BATCH_TILES)
+            ]
 
         ident_f32 = keep.tile([P, P], F32)
         make_identity(nc, ident_f32[:])
@@ -75,7 +89,7 @@ def tile_hyperlstmcell_pa_kernel(
         nc.vector.memset(w_scales[:].bitcast(I32), 0)
         gate_shift = keep.tile([P, GATES], F32)
         nc.vector.memset(gate_shift[:], 0.0)
-        nc.vector.memset(gate_shift[:, 1:2], 1.0)
+        nc.vector.memset(gate_shift[:, GATE_F : GATE_F + 1], 1.0)
         ones = keep.tile([P, P], BF16)
         nc.vector.memset(ones[:], 1.0)
         half = keep.tile([P, GATES], F32)
@@ -89,48 +103,75 @@ def tile_hyperlstmcell_pa_kernel(
         warm = keep.tile([P, 1], F32)
         nc.scalar.activation(out=warm[:], in_=gate_shift[:, 0:1], func=ACT.Sigmoid)
 
-        hh_sb = [keep.tile([P, UNITS], BF16, name="hh_sb%d" % t) for t in range(BATCH_TILES)]
-        hc_sb = [keep.tile([P, UNITS], BF16, name="hc_sb%d" % t) for t in range(BATCH_TILES)]
-        u_sb = [keep.tile([P, K], BF16, name="u_sb%d" % t) for t in range(BATCH_TILES)]
-
-        def load_rows(t):
-            rows = slice(t * P, (t + 1) * P)
-            nc.sync.dma_start(out=hh_sb[t][:], in_=hyper_h[rows, :])
-            nc.sync.dma_start(out=u_sb[t][:, 0:IN], in_=x[rows, :])
-            nc.sync.dma_start(out=u_sb[t][:, IN:K], in_=h[rows, :])
-            nc.sync.dma_start(out=hc_sb[t][:], in_=hyper_c[rows, :])
-
-        load_rows(0)
+        u_sb = per_tile("u_sb", [P, K], BF16)
+        hh_sb = per_tile("hh_sb", [P, UNITS], BF16)
+        hc_sb = per_tile("hc_sb", [P, UNITS], BF16)
         whh_sb = keep.tile([P, N // P, UNITS], BF16)
-        nc.sync.dma_start(out=whh_sb[:], in_=hc_Whh.rearrange("(c p) k -> p c k", p=P))
         w_words = keep.tile([P, PASSES, 2 * N], U8, align_bytes=64)
-        for g in range(PASSES):
-            nc.sync.dma_start(out=w_words[:, g, :].bitcast(I32), in_=hc_Wih_words[g].bitcast(I32))
+
+        def load_u(t):
+            nc.sync.dma_start(out=u_sb[t][:, 0:IN], in_=x[batch_rows(t), :])
+            nc.sync.dma_start(out=u_sb[t][:, IN:K], in_=h[batch_rows(t), :])
+
+        load_u(0)
+        nc.sync.dma_start(out=whh_sb[:], in_=hc_Whh.rearrange("(c p) k -> p c k", p=P))
+        nc.sync.dma_start(out=hh_sb[0][:], in_=hyper_h[batch_rows(0), :])
         for quad in range(4):
             nc.sync.dma_start(
                 out=w_scales[32 * quad : 32 * quad + 4, :, :].bitcast(I32),
                 in_=hc_Wih_scales[:, 4 * quad : 4 * quad + 4, :].bitcast(I32).rearrange("g r c -> r g c"),
             )
+        for g in range(PASSES):
+            nc.sync.dma_start(out=w_words[:, g, :].bitcast(I32), in_=hc_Wih_words[g].bitcast(I32))
         for t in range(1, BATCH_TILES):
-            load_rows(t)
+            nc.sync.dma_start(out=hh_sb[t][:], in_=hyper_h[batch_rows(t), :])
+            load_u(t)
+        for t in range(BATCH_TILES):
+            nc.sync.dma_start(out=hc_sb[t][:], in_=hyper_c[batch_rows(t), :])
 
-        hhT = [keep.tile([P, K_PLAIN, P], BF16, name="hhT%d" % t) for t in range(BATCH_TILES)]
-        u_codes = [keep.tile([P, PASSES * P], U32, name="u_codes%d" % t, align_bytes=64) for t in range(BATCH_TILES)]
-        u_scales = [keep.tile([P, PASSES * P], U8, name="u_scales%d" % t, align_bytes=64) for t in range(BATCH_TILES)]
-        plain = [keep.tile([P, N], F32, name="plain%d" % t) for t in range(BATCH_TILES)]
         whhT = keep.tile([P, K_PLAIN, N], BF16)
         gamma_bc = const_psum.tile([P, N], BF16)
         beta_bc = const_psum.tile([P, N], BF16)
         c_norm_bc = const_psum.tile([P, 2 * UNITS], BF16)
+        hhT = per_tile("hhT", [P, K_PLAIN, P], BF16)
+        grouped = per_tile("grouped", [P, PASSES, P, 4], BF16, align_bytes=64)
+        u_codes = per_tile("u_codes", [P, PASSES * P], U32, align_bytes=64)
+        u_scales = per_tile("u_scales", [P, PASSES * P], U8, align_bytes=64)
+        plain = per_tile("plain", [P, N], F32)
+        mx_banks = [None] * BATCH_TILES
+        v = per_tile("v", [P, N], F32)
+        sums = per_tile("sums", [P, GATES], F32)
+        scaled_sq = per_tile("scaled_sq", [P, GATES], F32)
+        root = per_tile("root", [P, GATES], F32)
+        std = per_tile("std", [P, GATES], F32)
+        inv = per_tile("inv", [P, GATES], F32)
+        neg_mean = per_tile("neg_mean", [P, GATES], F32)
+        centred = per_tile("centred", [P, N], F32)
+        normed = per_tile("normed", [P, N], F32)
+        act = per_tile("act", [P, N], F32)
+        kept = per_tile("kept", [P, UNITS], F32)
+        written = per_tile("written", [P, UNITS], F32)
+        raw_c = per_tile("raw_c", [P, UNITS], F32)
+        c_sum = per_tile("c_sum", [P, 1], F32)
+        c_scaled_sq = per_tile("c_scaled_sq", [P, 1], F32)
+        c_root = per_tile("c_root", [P, 1], F32)
+        c_std = per_tile("c_std", [P, 1], F32)
+        c_inv = per_tile("c_inv", [P, 1], F32)
+        c_neg_mean = per_tile("c_neg_mean", [P, 1], F32)
+        c_centred = per_tile("c_centred", [P, UNITS], F32)
+        new_c = per_tile("new_c", [P, UNITS], F32)
+        tanh_c = per_tile("tanh_c", [P, UNITS], F32)
+        new_h = per_tile("new_h", [P, UNITS], F32)
 
-        def transpose_rows(t):
+        def transpose_hh(t):
             hh_bank = work_psum.tile([P, K_PLAIN, P], BF16, tag="work")
             for kk in range(K_PLAIN):
                 nc.tensor.transpose(hh_bank[:, kk, :], hh_sb[t][:, kk * P : (kk + 1) * P], ident_bf16[:])
             nc.scalar.copy(out=hhT[t][:], in_=hh_bank[:])
+
+        def transpose_u(t):
             u_words = u_sb[t][:].bitcast(F32)
-            grouped = stage.tile([P, PASSES, P, 4], BF16, align_bytes=64)
-            grouped_words = grouped[:].bitcast(F32)
+            grouped_words = grouped[t][:].bitcast(F32)
             for pair in range(PASSES // 2):
                 planes = work_psum.tile([P, 2, 2, P], F32, tag="work")
                 for gg in range(2):
@@ -143,13 +184,12 @@ def tile_hyperlstmcell_pa_kernel(
                     out=grouped_words[:, 2 * pair : 2 * pair + 2, :, :],
                     in_=planes[:].rearrange("p g w b -> p g b w"),
                 )
-            return grouped
 
-        def quantise(t, grouped):
+        def quantise(t):
             nc.vector.quantize_mx(
                 out=u_codes[t][:].bitcast(FP8X4),
                 scales=u_scales[t][:],
-                in_=grouped[:].rearrange("p g b j -> p (g b j)"),
+                in_=grouped[t][:].rearrange("p g b j -> p (g b j)"),
             )
 
         def plain_product(t):
@@ -162,13 +202,12 @@ def tile_hyperlstmcell_pa_kernel(
                 nc.scalar.copy(out=plain[t][:, cols], in_=acc[:])
 
         def mx_product(t):
-            banks = []
-            for half_n in range(HALVES):
-                acc = mx_psum.tile([P, BANK], F32, tag="mx", name="mx_acc")
-                for g in range(PASSES):
-                    rows = slice(g * P, (g + 1) * P)
+            mx_banks[t] = [mx_psum.tile([P, BANK], F32, tag="mx", name="mx_acc") for half_n in range(HALVES)]
+            for g in range(PASSES):
+                rows = slice(g * P, (g + 1) * P)
+                for half_n in range(HALVES):
                     nc.tensor.matmul_mx(
-                        out=acc[:],
+                        out=mx_banks[t][half_n][:],
                         lhsT=u_codes[t][:, rows].bitcast(FP8X4),
                         lhsT_scale=u_scales[t][:, rows],
                         rhs=w_words[:, g, 2 * half_n * BANK : 2 * (half_n + 1) * BANK].bitcast(FP4X4),
@@ -176,126 +215,115 @@ def tile_hyperlstmcell_pa_kernel(
                         start=(g == 0),
                         stop=(g == PASSES - 1),
                     )
-                banks.append(acc)
-            return banks
 
-        def std_plus_eps(scaled_sq, width, tag):
-            root = stats.tile([P, width], F32, tag=tag + "_root")
-            nc.gpsimd.tensor_tensor(out=root[:], in0=scaled_sq[:], in1=half[:, 0:width], op=ALU.pow)
-            std = stats.tile([P, width], F32, tag=tag + "_std")
-            nc.gpsimd.tensor_scalar(
-                out=std[:], in0=root[:], scalar1=ROOT_TO_STD, scalar2=EPS, op0=ALU.mult, op1=ALU.add
+        def sum_of_squares(values, total, out):
+            squares = scrap.tile([P, UNITS], F32, tag="squares")
+            nc.scalar.activation(
+                out=squares[:], in_=values, func=ACT.Square, scale=-float(UNITS), bias=total, accum_out=out
             )
-            return std
 
-        def join_and_centre(t, banks):
-            v = post.tile([P, N], F32, tag="v")
-            sums = stats.tile([P, GATES], F32, tag="sums")
-            scaled_sq = stats.tile([P, GATES], F32, tag="scaled_sq")
+        def std_plus_eps(sq, sq_root, out):
+            width = sq.shape[1]
+            nc.gpsimd.tensor_tensor(out=sq_root, in0=sq, in1=half[:, 0:width], op=ALU.pow)
+            nc.gpsimd.tensor_scalar(
+                out=out, in0=sq_root, scalar1=ROOT_TO_STD, scalar2=EPS, op0=ALU.mult, op1=ALU.add
+            )
+
+        def join(t):
             for j in range(GATES):
-                in_bank = gate_cols(j % GATES_PER_BANK)
                 nc.vector.scalar_tensor_tensor(
-                    out=v[:, gate_cols(j)],
-                    in0=banks[j // GATES_PER_BANK][:, in_bank],
+                    out=v[t][:, gate_cols(j)],
+                    in0=mx_banks[t][j // GATES_PER_BANK][:, gate_cols(j % GATES_PER_BANK)],
                     scalar=1.0,
                     in1=plain[t][:, gate_cols(j)],
                     op0=ALU.mult,
                     op1=ALU.add,
-                    accum_out=sums[:, j : j + 1],
+                    accum_out=sums[t][:, j : j + 1],
                 )
-                squares = post.tile([P, UNITS], F32, tag="squares")
-                nc.scalar.activation(
-                    out=squares[:],
-                    in_=v[:, gate_cols(j)],
-                    func=ACT.Square,
-                    scale=-float(UNITS),
-                    bias=sums[:, j : j + 1],
-                    accum_out=scaled_sq[:, j : j + 1],
-                )
-            std = std_plus_eps(scaled_sq, GATES, "gate")
-            neg_mean = stats.tile([P, GATES], F32, tag="neg_mean")
-            nc.vector.tensor_scalar_mul(out=neg_mean[:], in0=sums[:], scalar1=-1.0 / UNITS)
-            centred = post.tile([P, N], F32, tag="centred")
-            for j in range(GATES):
-                nc.vector.scalar_tensor_tensor(
-                    out=centred[:, gate_cols(j)],
-                    in0=v[:, gate_cols(j)],
-                    scalar=neg_mean[:, j : j + 1],
-                    in1=gamma_bc[:, gate_cols(j)],
-                    op0=ALU.add,
-                    op1=ALU.mult,
-                )
-            return centred, std
+                sum_of_squares(v[t][:, gate_cols(j)], sums[t][:, j : j + 1], scaled_sq[t][:, j : j + 1])
 
-        def activate(centred, std):
-            inv = stats.tile([P, GATES], F32, tag="inv")
-            nc.vector.reciprocal(out=inv[:], in_=std[:])
-            normed = post.tile([P, N], F32, tag="normed")
-            act = post.tile([P, N], F32, tag="act")
-            for j, func in enumerate((ACT.Sigmoid, ACT.Sigmoid, ACT.Tanh, ACT.Sigmoid)):
-                nc.vector.scalar_tensor_tensor(
-                    out=normed[:, gate_cols(j)],
-                    in0=centred[:, gate_cols(j)],
-                    scalar=inv[:, j : j + 1],
-                    in1=beta_bc[:, gate_cols(j)],
-                    op0=ALU.mult,
-                    op1=ALU.add,
-                )
-                nc.scalar.activation(
-                    out=act[:, gate_cols(j)], in_=normed[:, gate_cols(j)], func=func, bias=gate_shift[:, j : j + 1]
-                )
-            return act
+        def gate_mean(t):
+            nc.vector.tensor_scalar_mul(out=neg_mean[t][:], in0=sums[t][:], scalar1=-1.0 / UNITS)
 
-        def cell_sum(t, act):
-            kept = post.tile([P, UNITS], F32, tag="kept")
-            nc.vector.tensor_tensor(out=kept[:], in0=hc_sb[t][:], in1=act[:, gate_cols(1)], op=ALU.mult)
-            written = post.tile([P, UNITS], F32, tag="written")
-            nc.vector.tensor_tensor(out=written[:], in0=act[:, gate_cols(0)], in1=act[:, gate_cols(2)], op=ALU.mult)
-            raw_c = post.tile([P, UNITS], F32, tag="raw_c")
-            c_sum = stats.tile([P, 1], F32, tag="c_sum")
+        def centre_gate(t, j):
             nc.vector.scalar_tensor_tensor(
-                out=raw_c[:], in0=kept[:], scalar=1.0, in1=written[:], op0=ALU.mult, op1=ALU.add, accum_out=c_sum[:]
+                out=centred[t][:, gate_cols(j)],
+                in0=v[t][:, gate_cols(j)],
+                scalar=neg_mean[t][:, j : j + 1],
+                in1=gamma_bc[:, gate_cols(j)],
+                op0=ALU.add,
+                op1=ALU.mult,
             )
-            c_scaled_sq = stats.tile([P, 1], F32, tag="c_scaled_sq")
-            c_squares = post.tile([P, UNITS], F32, tag="squares")
+
+        def norm_gate(t, j):
+            nc.vector.scalar_tensor_tensor(
+                out=normed[t][:, gate_cols(j)],
+                in0=centred[t][:, gate_cols(j)],
+                scalar=inv[t][:, j : j + 1],
+                in1=beta_bc[:, gate_cols(j)],
+                op0=ALU.mult,
+                op1=ALU.add,
+            )
+
+        def squash_gate(t, j):
             nc.scalar.activation(
-                out=c_squares[:],
-                in_=raw_c[:],
-                func=ACT.Square,
-                scale=-float(UNITS),
-                bias=c_sum[:],
-                accum_out=c_scaled_sq[:],
+                out=act[t][:, gate_cols(j)],
+                in_=normed[t][:, gate_cols(j)],
+                func=GATE_FUNC[j],
+                bias=gate_shift[:, j : j + 1],
             )
-            c_std = std_plus_eps(c_scaled_sq, 1, "cell")
-            c_neg_mean = stats.tile([P, 1], F32, tag="c_neg_mean")
-            nc.vector.tensor_scalar_mul(out=c_neg_mean[:], in0=c_sum[:], scalar1=-1.0 / UNITS)
-            c_centred = post.tile([P, UNITS], F32, tag="c_centred")
-            nc.vector.scalar_tensor_tensor(
-                out=c_centred[:], in0=raw_c[:], scalar=c_neg_mean[:], in1=c_norm_bc[:, 0:UNITS], op0=ALU.add, op1=ALU.mult
-            )
-            return c_centred, c_std
 
-        def cell_finish(t, c_centred, c_std, act):
-            rows = slice(t * P, (t + 1) * P)
-            c_inv = stats.tile([P, 1], F32, tag="c_inv")
-            nc.vector.reciprocal(out=c_inv[:], in_=c_std[:])
-            new_c = post.tile([P, UNITS], F32, tag="new_c")
-            nc.vector.scalar_tensor_tensor(
-                out=new_c[:], in0=c_centred[:], scalar=c_inv[:], in1=c_norm_bc[:, UNITS : 2 * UNITS], op0=ALU.mult, op1=ALU.add
+        def cell_products(t):
+            nc.vector.tensor_tensor(out=kept[t][:], in0=hc_sb[t][:], in1=act[t][:, gate_cols(GATE_F)], op=ALU.mult)
+            nc.vector.tensor_tensor(
+                out=written[t][:], in0=act[t][:, gate_cols(GATE_I)], in1=act[t][:, gate_cols(GATE_G)], op=ALU.mult
             )
-            nc.sync.dma_start(out=out_1[rows, :], in_=new_c[:])
-            tanh_c = post.tile([P, UNITS], F32, tag="tanh_c")
-            nc.scalar.activation(out=tanh_c[:], in_=new_c[:], func=ACT.Tanh)
-            new_h = post.tile([P, UNITS], F32, tag="new_h")
-            nc.vector.tensor_tensor(out=new_h[:], in0=tanh_c[:], in1=act[:, gate_cols(3)], op=ALU.mult)
-            nc.sync.dma_start(out=out_0[rows, :], in_=new_h[:])
+
+        def cell_sum(t):
+            nc.vector.scalar_tensor_tensor(
+                out=raw_c[t][:],
+                in0=kept[t][:],
+                scalar=1.0,
+                in1=written[t][:],
+                op0=ALU.mult,
+                op1=ALU.add,
+                accum_out=c_sum[t][:],
+            )
+
+        def cell_mean(t):
+            nc.vector.tensor_scalar_mul(out=c_neg_mean[t][:], in0=c_sum[t][:], scalar1=-1.0 / UNITS)
+
+        def centre_cell(t):
+            nc.vector.scalar_tensor_tensor(
+                out=c_centred[t][:],
+                in0=raw_c[t][:],
+                scalar=c_neg_mean[t][:],
+                in1=c_norm_bc[:, 0:UNITS],
+                op0=ALU.add,
+                op1=ALU.mult,
+            )
+
+        def norm_cell(t):
+            nc.vector.scalar_tensor_tensor(
+                out=new_c[t][:],
+                in0=c_centred[t][:],
+                scalar=c_inv[t][:],
+                in1=c_norm_bc[:, UNITS : 2 * UNITS],
+                op0=ALU.mult,
+                op1=ALU.add,
+            )
+            nc.sync.dma_start(out=out_1[batch_rows(t), :], in_=new_c[t][:])
+
+        def hidden(t):
+            nc.vector.tensor_tensor(out=new_h[t][:], in0=tanh_c[t][:], in1=act[t][:, gate_cols(GATE_O)], op=ALU.mult)
+            nc.sync.dma_start(out=out_0[batch_rows(t), :], in_=new_h[t][:])
 
         norm_cols_bank = work_psum.tile([P, P], BF16, tag="work")
         nc.tensor.transpose(norm_cols_bank[:], norm_rows[:], ident_bf16[:])
         norm_cols = keep.tile([P, 20], BF16)
         nc.vector.tensor_copy(out=norm_cols[:], in_=norm_cols_bank[:, 0:20])
-        grouped = transpose_rows(0)
-        quantise(0, grouped)
+        transpose_u(0)
+        quantise(0)
         for kk in range(K_PLAIN):
             whh_bank = work_psum.tile([P, N], BF16, tag="work")
             for c in range(N // P):
@@ -303,6 +331,7 @@ def tile_hyperlstmcell_pa_kernel(
                     whh_bank[:, c * P : (c + 1) * P], whh_sb[:, c, kk * P : (kk + 1) * P], ident_bf16[:]
                 )
             nc.vector.tensor_copy(out=whhT[:, kk, :], in_=whh_bank[:])
+        transpose_hh(0)
         for first, spread in ((0, gamma_bc), (8, beta_bc), (16, c_norm_bc)):
             for c in range(spread.shape[1] // P):
                 nc.tensor.transpose(
@@ -311,22 +340,52 @@ def tile_hyperlstmcell_pa_kernel(
                     ident_bf16[:],
                 )
         plain_product(0)
-        banks = mx_product(0)
+        mx_product(0)
 
-        act = None
-        for t in range(BATCH_TILES + 1):
-            if t + 1 < BATCH_TILES:
-                grouped = transpose_rows(t + 1)
-            if t < BATCH_TILES:
-                centred, std = join_and_centre(t, banks)
-            if t + 1 < BATCH_TILES:
-                quantise(t + 1, grouped)
-                plain_product(t + 1)
-                banks = mx_product(t + 1)
-            if t >= 1:
-                c_centred, c_std = cell_sum(t - 1, act)
-            older_act = act
-            if t < BATCH_TILES:
-                act = activate(centred, std)
-            if t >= 1:
-                cell_finish(t - 1, c_centred, c_std, older_act)
+        for r in range(BATCH_TILES + 2):
+            ahead, now, cell, last = r + 1, r, r - 1, r - 2
+            if live(ahead):
+                transpose_hh(ahead)
+            if live(now):
+                join(now)
+                std_plus_eps(scaled_sq[now][:], root[now][:], std[now][:])
+            if live(ahead):
+                transpose_u(ahead)
+            if live(cell):
+                cell_products(cell)
+            if live(now):
+                gate_mean(now)
+            if live(cell):
+                cell_sum(cell)
+            if live(now):
+                for j in CELL_GATES:
+                    centre_gate(now, j)
+            if live(ahead):
+                quantise(ahead)
+            if live(last):
+                nc.scalar.activation(out=tanh_c[last][:], in_=new_c[last][:], func=ACT.Tanh)
+                hidden(last)
+            if live(cell):
+                squash_gate(cell, GATE_O)
+                sum_of_squares(raw_c[cell][:], c_sum[cell][:], c_scaled_sq[cell][:])
+                std_plus_eps(c_scaled_sq[cell][:], c_root[cell][:], c_std[cell][:])
+                cell_mean(cell)
+            if live(now):
+                centre_gate(now, GATE_O)
+            if live(ahead):
+                plain_product(ahead)
+                mx_product(ahead)
+            if live(now):
+                nc.vector.reciprocal(out=inv[now][:], in_=std[now][:])
+            if live(cell):
+                centre_cell(cell)
+            if live(now):
+                for j in CELL_GATES:
+                    norm_gate(now, j)
+                    squash_gate(now, j)
+            if live(cell):
+                nc.vector.reciprocal(out=c_inv[cell][:], in_=c_std[cell][:])
+            if live(now):
+                norm_gate(now, GATE_O)
+            if live(cell):
+                norm_cell(cell)

@@ -25,6 +25,7 @@ HALVES = N // BANK
 GATES_PER_BANK = BANK // UNITS
 BATCH_TILES = BATCH // P
 K_PLAIN = UNITS // P
+RUN = 4
 EPS = 1e-6
 ROOT_TO_STD = 1.0 / (UNITS * math.sqrt(UNITS - 1))
 GATE_I, GATE_F, GATE_G, GATE_O = 0, 1, 2, 3
@@ -325,20 +326,24 @@ def tile_hyperlstmcell_pa_kernel(
         transpose_u(0)
         quantise(0)
         for kk in range(K_PLAIN):
-            whh_bank = work_psum.tile([P, N], BF16, tag="work")
-            for c in range(N // P):
-                nc.tensor.transpose(
-                    whh_bank[:, c * P : (c + 1) * P], whh_sb[:, c, kk * P : (kk + 1) * P], ident_bf16[:]
+            for run in range(N // P // RUN):
+                whh_bank = work_psum.tile([P, RUN, P], BF16, tag="work")
+                for i in range(RUN):
+                    nc.tensor.transpose(
+                        whh_bank[:, i, :], whh_sb[:, run * RUN + i, kk * P : (kk + 1) * P], ident_bf16[:]
+                    )
+                nc.vector.tensor_copy(
+                    out=whhT[:, kk, run * RUN * P : (run + 1) * RUN * P], in_=whh_bank[:].rearrange("p i n -> p (i n)")
                 )
-            nc.vector.tensor_copy(out=whhT[:, kk, :], in_=whh_bank[:])
         transpose_hh(0)
-        for first, spread in ((0, gamma_bc), (8, beta_bc), (16, c_norm_bc)):
-            for c in range(spread.shape[1] // P):
-                nc.tensor.transpose(
-                    spread[:, c * P : (c + 1) * P],
-                    norm_cols[:, first + c : first + c + 1].to_broadcast([P, P]),
-                    ident_bf16[:],
-                )
+        for run in range(N // P // RUN):
+            for first, spread in ((0, gamma_bc), (8, beta_bc), (16, c_norm_bc)):
+                for c in range(run * RUN, min((run + 1) * RUN, spread.shape[1] // P)):
+                    nc.tensor.transpose(
+                        spread[:, c * P : (c + 1) * P],
+                        norm_cols[:, first + c : first + c + 1].to_broadcast([P, P]),
+                        ident_bf16[:],
+                    )
         plain_product(0)
         mx_product(0)
 

@@ -130,11 +130,11 @@ def tile_hyperlstmcell_pa_kernel(
         for t in range(BATCH_TILES):
             nc.sync.dma_start(out=hc_sb[t][:], in_=hyper_c[batch_rows(t), :])
 
-        whhT = keep.tile([P, K_PLAIN, N], BF16)
+        whhT = keep.tile([P, N, K_PLAIN], BF16)
         gamma_bc = const_psum.tile([P, N], BF16)
         beta_bc = const_psum.tile([P, N], BF16)
         c_norm_bc = const_psum.tile([P, 2 * UNITS], BF16)
-        hhT = per_tile("hhT", [P, K_PLAIN, P], BF16)
+        hhT = per_tile("hhT", [P, P, K_PLAIN], BF16)
         grouped = per_tile("grouped", [P, PASSES, P, 4], BF16, align_bytes=64)
         u_codes = per_tile("u_codes", [P, PASSES * P], U32, align_bytes=64)
         u_scales = per_tile("u_scales", [P, PASSES * P], U8, align_bytes=64)
@@ -165,10 +165,9 @@ def tile_hyperlstmcell_pa_kernel(
         new_h = per_tile("new_h", [P, UNITS], F32)
 
         def transpose_hh(t):
-            hh_bank = work_psum.tile([P, K_PLAIN, P], BF16, tag="work")
-            for kk in range(K_PLAIN):
-                nc.tensor.transpose(hh_bank[:, kk, :], hh_sb[t][:, kk * P : (kk + 1) * P], ident_bf16[:])
-            nc.scalar.copy(out=hhT[t][:], in_=hh_bank[:])
+            hh_bank = work_psum.tile([P, P], F32, tag="work")
+            nc.tensor.transpose(hh_bank[:], hh_sb[t][:].bitcast(F32), ident_f32[:])
+            nc.scalar.copy(out=hhT[t][:].rearrange("p b e -> p (b e)"), in_=hh_bank[:].bitcast(BF16))
 
         def transpose_u(t):
             u_words = u_sb[t][:].bitcast(F32)
@@ -197,8 +196,8 @@ def tile_hyperlstmcell_pa_kernel(
             for half_n in range(HALVES):
                 cols = slice(half_n * BANK, (half_n + 1) * BANK)
                 acc = work_psum.tile([P, BANK], F32, tag="work")
-                for kk in range(K_PLAIN):
-                    nc.tensor.matmul(acc[:], lhsT=hhT[t][:, kk, :], rhs=whhT[:, kk, cols], start=(kk == 0), stop=False)
+                for e in range(K_PLAIN):
+                    nc.tensor.matmul(acc[:], lhsT=hhT[t][:, :, e], rhs=whhT[:, cols, e], start=(e == 0), stop=False)
                 nc.tensor.matmul(acc[:], lhsT=ones[:], rhs=bias_row[:, cols], start=False, stop=True)
                 nc.scalar.copy(out=plain[t][:, cols], in_=acc[:])
 
@@ -324,26 +323,28 @@ def tile_hyperlstmcell_pa_kernel(
         norm_cols = keep.tile([P, 20], BF16)
         nc.vector.tensor_copy(out=norm_cols[:], in_=norm_cols_bank[:, 0:20])
         transpose_u(0)
-        quantise(0)
-        for kk in range(K_PLAIN):
-            for run in range(N // P // RUN):
-                whh_bank = work_psum.tile([P, RUN, P], BF16, tag="work")
-                for i in range(RUN):
-                    nc.tensor.transpose(
-                        whh_bank[:, i, :], whh_sb[:, run * RUN + i, kk * P : (kk + 1) * P], ident_bf16[:]
-                    )
-                nc.vector.tensor_copy(
-                    out=whhT[:, kk, run * RUN * P : (run + 1) * RUN * P], in_=whh_bank[:].rearrange("p i n -> p (i n)")
-                )
-        transpose_hh(0)
+        whh_words = whh_sb[:].bitcast(F32)
         for run in range(N // P // RUN):
-            for first, spread in ((0, gamma_bc), (8, beta_bc), (16, c_norm_bc)):
-                for c in range(run * RUN, min((run + 1) * RUN, spread.shape[1] // P)):
-                    nc.tensor.transpose(
-                        spread[:, c * P : (c + 1) * P],
-                        norm_cols[:, first + c : first + c + 1].to_broadcast([P, P]),
-                        ident_bf16[:],
-                    )
+            whh_bank = work_psum.tile([P, RUN, P], F32, tag="work")
+            for i in range(RUN):
+                nc.tensor.transpose(whh_bank[:, i, :], whh_words[:, run * RUN + i, :], ident_f32[:])
+            nc.vector.tensor_copy(
+                out=whhT[:, run * RUN * P : (run + 1) * RUN * P, :].rearrange("p n e -> p (n e)"),
+                in_=whh_bank[:].rearrange("p i n -> p (i n)").bitcast(BF16),
+            )
+        quantise(0)
+        transpose_hh(0)
+
+        def spread_over_partitions(first, spread):
+            for c in range(spread.shape[1] // P):
+                nc.tensor.transpose(
+                    spread[:, c * P : (c + 1) * P],
+                    norm_cols[:, first + c : first + c + 1].to_broadcast([P, P]),
+                    ident_bf16[:],
+                )
+
+        to_spread = [(0, gamma_bc), (8, beta_bc), (16, c_norm_bc)]
+        spread_over_partitions(*to_spread[0])
         plain_product(0)
         mx_product(0)
 
@@ -379,6 +380,9 @@ def tile_hyperlstmcell_pa_kernel(
                 centre_gate(now, GATE_O)
             if live(ahead):
                 plain_product(ahead)
+            if ahead < len(to_spread):
+                spread_over_partitions(*to_spread[ahead])
+            if live(ahead):
                 mx_product(ahead)
             if live(now):
                 nc.vector.reciprocal(out=inv[now][:], in_=std[now][:])

@@ -78,16 +78,12 @@ def tile_hyperlstmcell_pa_kernel(
                 keep.tile(shape, dtype, name="%s%d" % (name, t), align_bytes=align_bytes) for t in range(BATCH_TILES)
             ]
 
-        ident_f32 = keep.tile([P, P], F32)
-        make_identity(nc, ident_f32[:])
-        ident_bf16 = keep.tile([P, P], BF16)
-        make_identity(nc, ident_bf16[:])
-        norm_rows = keep.tile([P, P], BF16)
-        nc.vector.memset(norm_rows[:], 0.0)
         bias_row = keep.tile([P, N], BF16)
         nc.vector.memset(bias_row[:], 0.0)
         w_scales = keep.tile([P, PASSES, N], U8, align_bytes=64)
         nc.vector.memset(w_scales[:].bitcast(I32), 0)
+        norm_rows = keep.tile([P, P], BF16)
+        nc.vector.memset(norm_rows[:], 0.0)
         gate_shift = keep.tile([P, GATES], F32)
         nc.vector.memset(gate_shift[:], 0.0)
         nc.vector.memset(gate_shift[:, GATE_F : GATE_F + 1], 1.0)
@@ -96,39 +92,58 @@ def tile_hyperlstmcell_pa_kernel(
         half = keep.tile([P, GATES], F32)
         nc.vector.memset(half[:], 0.5)
 
-        nc.scalar.dma_start(out=norm_rows[0:8, :], in_=hc_ln_gamma.rearrange("g (c n) -> (g c) n", n=P))
-        nc.scalar.dma_start(out=norm_rows[8:16, :], in_=hc_ln_beta.rearrange("g (c n) -> (g c) n", n=P))
-        nc.scalar.dma_start(out=norm_rows[16:18, :], in_=hc_lnc_gamma.rearrange("(c n) -> c n", n=P))
-        nc.scalar.dma_start(out=norm_rows[18:20, :], in_=hc_lnc_beta.rearrange("(c n) -> c n", n=P))
-        nc.scalar.dma_start(out=bias_row[0:1, :], in_=hc_bih.unsqueeze(0))
         warm = keep.tile([P, 1], F32)
         nc.scalar.activation(out=warm[:], in_=gate_shift[:, 0:1], func=ACT.Sigmoid)
 
         u_sb = per_tile("u_sb", [P, K], BF16)
-        hh_sb = per_tile("hh_sb", [P, UNITS], BF16)
-        hc_sb = per_tile("hc_sb", [P, UNITS], BF16)
+        hh_sb = keep.tile([P, BATCH_TILES, UNITS], BF16)
+        hc_sb = keep.tile([P, BATCH_TILES, UNITS], BF16)
         whh_sb = keep.tile([P, N // P, UNITS], BF16)
-        w_words = keep.tile([P, PASSES, 2 * N], U8, align_bytes=64)
+        w_words = [
+            keep.tile([P, PASSES, 2 * BANK], U8, name="w_words%d" % half_n, align_bytes=64) for half_n in range(HALVES)
+        ]
 
         def load_u(t):
             nc.sync.dma_start(out=u_sb[t][:, 0:IN], in_=x[batch_rows(t), :])
             nc.sync.dma_start(out=u_sb[t][:, IN:K], in_=h[batch_rows(t), :])
 
+        def load_whh(half_n):
+            chunks = slice(half_n * BANK // P, (half_n + 1) * BANK // P)
+            nc.sync.dma_start(
+                out=whh_sb[:, chunks, :],
+                in_=hc_Whh[half_n * BANK : (half_n + 1) * BANK, :].rearrange("(c p) k -> p c k", p=P),
+            )
+
+        def load_w_words(half_n):
+            some = slice(2 * half_n * BANK, 2 * (half_n + 1) * BANK)
+            nc.sync.dma_start(
+                out=w_words[half_n][:].bitcast(I32),
+                in_=hc_Wih_words[:, :, some].bitcast(I32).rearrange("g p c -> p g c"),
+            )
+
+        nc.gpsimd.dma_start(out=hh_sb[:], in_=hyper_h.rearrange("(t p) k -> p t k", p=P))
+        nc.gpsimd.dma_start(out=bias_row[0:1, :], in_=hc_bih.unsqueeze(0))
+        ident_f32 = keep.tile([P, P], F32)
+        make_identity(nc, ident_f32[:])
+        ident_bf16 = keep.tile([P, P], BF16)
+        make_identity(nc, ident_bf16[:])
         load_u(0)
-        nc.sync.dma_start(out=whh_sb[:], in_=hc_Whh.rearrange("(c p) k -> p c k", p=P))
-        nc.sync.dma_start(out=hh_sb[0][:], in_=hyper_h[batch_rows(0), :])
+        load_whh(0)
         for quad in range(4):
             nc.sync.dma_start(
                 out=w_scales[32 * quad : 32 * quad + 4, :, :].bitcast(I32),
                 in_=hc_Wih_scales[:, 4 * quad : 4 * quad + 4, :].bitcast(I32).rearrange("g r c -> r g c"),
             )
-        for g in range(PASSES):
-            nc.sync.dma_start(out=w_words[:, g, :].bitcast(I32), in_=hc_Wih_words[g].bitcast(I32))
+        load_w_words(0)
+        load_whh(1)
+        load_w_words(1)
+        nc.sync.dma_start(out=norm_rows[0:8, :], in_=hc_ln_gamma.rearrange("g (c n) -> (g c) n", n=P))
+        nc.sync.dma_start(out=norm_rows[8:16, :], in_=hc_ln_beta.rearrange("g (c n) -> (g c) n", n=P))
+        nc.sync.dma_start(out=norm_rows[16:18, :], in_=hc_lnc_gamma.rearrange("(c n) -> c n", n=P))
+        nc.sync.dma_start(out=norm_rows[18:20, :], in_=hc_lnc_beta.rearrange("(c n) -> c n", n=P))
         for t in range(1, BATCH_TILES):
-            nc.sync.dma_start(out=hh_sb[t][:], in_=hyper_h[batch_rows(t), :])
             load_u(t)
-        for t in range(BATCH_TILES):
-            nc.sync.dma_start(out=hc_sb[t][:], in_=hyper_c[batch_rows(t), :])
+        nc.sync.dma_start(out=hc_sb[:], in_=hyper_c.rearrange("(t p) k -> p t k", p=P))
 
         whhT = keep.tile([P, N, K_PLAIN], BF16)
         gamma_bc = const_psum.tile([P, N], BF16)
@@ -139,7 +154,7 @@ def tile_hyperlstmcell_pa_kernel(
         u_codes = per_tile("u_codes", [P, PASSES * P], U32, align_bytes=64)
         u_scales = per_tile("u_scales", [P, PASSES * P], U8, align_bytes=64)
         plain = per_tile("plain", [P, N], F32)
-        mx_banks = [None] * BATCH_TILES
+        mx_banks = [[] for t in range(BATCH_TILES)]
         v = per_tile("v", [P, N], F32)
         sums = per_tile("sums", [P, GATES], F32)
         scaled_sq = per_tile("scaled_sq", [P, GATES], F32)
@@ -166,7 +181,7 @@ def tile_hyperlstmcell_pa_kernel(
 
         def transpose_hh(t):
             hh_bank = work_psum.tile([P, P], F32, tag="work")
-            nc.tensor.transpose(hh_bank[:], hh_sb[t][:].bitcast(F32), ident_f32[:])
+            nc.tensor.transpose(hh_bank[:], hh_sb[:, t, :].bitcast(F32), ident_f32[:])
             nc.scalar.copy(out=hhT[t][:].rearrange("p b e -> p (b e)"), in_=hh_bank[:].bitcast(BF16))
 
         def transpose_u(t):
@@ -192,29 +207,28 @@ def tile_hyperlstmcell_pa_kernel(
                 in_=grouped[t][:].rearrange("p g b j -> p (g b j)"),
             )
 
-        def plain_product(t):
-            for half_n in range(HALVES):
-                cols = slice(half_n * BANK, (half_n + 1) * BANK)
-                acc = work_psum.tile([P, BANK], F32, tag="work")
-                for e in range(K_PLAIN):
-                    nc.tensor.matmul(acc[:], lhsT=hhT[t][:, :, e], rhs=whhT[:, cols, e], start=(e == 0), stop=False)
-                nc.tensor.matmul(acc[:], lhsT=ones[:], rhs=bias_row[:, cols], start=False, stop=True)
-                nc.scalar.copy(out=plain[t][:, cols], in_=acc[:])
+        def plain_product(t, half_n):
+            cols = slice(half_n * BANK, (half_n + 1) * BANK)
+            acc = work_psum.tile([P, BANK], F32, tag="work")
+            for e in range(K_PLAIN):
+                nc.tensor.matmul(acc[:], lhsT=hhT[t][:, :, e], rhs=whhT[:, cols, e], start=(e == 0), stop=False)
+            nc.tensor.matmul(acc[:], lhsT=ones[:], rhs=bias_row[:, cols], start=False, stop=True)
+            nc.scalar.copy(out=plain[t][:, cols], in_=acc[:])
 
-        def mx_product(t):
-            mx_banks[t] = [mx_psum.tile([P, BANK], F32, tag="mx", name="mx_acc") for half_n in range(HALVES)]
+        def mx_product(t, half_n):
+            bank = mx_psum.tile([P, BANK], F32, tag="mx", name="mx_acc")
+            mx_banks[t].append(bank)
             for g in range(PASSES):
                 rows = slice(g * P, (g + 1) * P)
-                for half_n in range(HALVES):
-                    nc.tensor.matmul_mx(
-                        out=mx_banks[t][half_n][:],
-                        lhsT=u_codes[t][:, rows].bitcast(FP8X4),
-                        lhsT_scale=u_scales[t][:, rows],
-                        rhs=w_words[:, g, 2 * half_n * BANK : 2 * (half_n + 1) * BANK].bitcast(FP4X4),
-                        rhs_scale=w_scales[:, g, half_n * BANK : (half_n + 1) * BANK],
-                        start=(g == 0),
-                        stop=(g == PASSES - 1),
-                    )
+                nc.tensor.matmul_mx(
+                    out=bank[:],
+                    lhsT=u_codes[t][:, rows].bitcast(FP8X4),
+                    lhsT_scale=u_scales[t][:, rows],
+                    rhs=w_words[half_n][:, g, :].bitcast(FP4X4),
+                    rhs_scale=w_scales[:, g, half_n * BANK : (half_n + 1) * BANK],
+                    start=(g == 0),
+                    stop=(g == PASSES - 1),
+                )
 
         def sum_of_squares(values, total, out):
             squares = scrap.tile([P, UNITS], F32, tag="squares")
@@ -229,11 +243,11 @@ def tile_hyperlstmcell_pa_kernel(
                 out=out, in0=sq_root, scalar1=ROOT_TO_STD, scalar2=EPS, op0=ALU.mult, op1=ALU.add
             )
 
-        def join(t):
-            for j in range(GATES):
+        def join(t, half_n):
+            for j in range(half_n * GATES_PER_BANK, (half_n + 1) * GATES_PER_BANK):
                 nc.vector.scalar_tensor_tensor(
                     out=v[t][:, gate_cols(j)],
-                    in0=mx_banks[t][j // GATES_PER_BANK][:, gate_cols(j % GATES_PER_BANK)],
+                    in0=mx_banks[t][half_n][:, gate_cols(j % GATES_PER_BANK)],
                     scalar=1.0,
                     in1=plain[t][:, gate_cols(j)],
                     op0=ALU.mult,
@@ -274,7 +288,7 @@ def tile_hyperlstmcell_pa_kernel(
             )
 
         def cell_products(t):
-            nc.vector.tensor_tensor(out=kept[t][:], in0=hc_sb[t][:], in1=act[t][:, gate_cols(GATE_F)], op=ALU.mult)
+            nc.vector.tensor_tensor(out=kept[t][:], in0=hc_sb[:, t, :], in1=act[t][:, gate_cols(GATE_F)], op=ALU.mult)
             nc.vector.tensor_tensor(
                 out=written[t][:], in0=act[t][:, gate_cols(GATE_I)], in1=act[t][:, gate_cols(GATE_G)], op=ALU.mult
             )
@@ -318,22 +332,16 @@ def tile_hyperlstmcell_pa_kernel(
             nc.vector.tensor_tensor(out=new_h[t][:], in0=tanh_c[t][:], in1=act[t][:, gate_cols(GATE_O)], op=ALU.mult)
             nc.sync.dma_start(out=out_0[batch_rows(t), :], in_=new_h[t][:])
 
-        norm_cols_bank = work_psum.tile([P, P], BF16, tag="work")
-        nc.tensor.transpose(norm_cols_bank[:], norm_rows[:], ident_bf16[:])
-        norm_cols = keep.tile([P, 20], BF16)
-        nc.vector.tensor_copy(out=norm_cols[:], in_=norm_cols_bank[:, 0:20])
-        transpose_u(0)
         whh_words = whh_sb[:].bitcast(F32)
-        for run in range(N // P // RUN):
+
+        def transpose_whh(half_n):
             whh_bank = work_psum.tile([P, RUN, P], F32, tag="work")
             for i in range(RUN):
-                nc.tensor.transpose(whh_bank[:, i, :], whh_words[:, run * RUN + i, :], ident_f32[:])
+                nc.tensor.transpose(whh_bank[:, i, :], whh_words[:, half_n * RUN + i, :], ident_f32[:])
             nc.vector.tensor_copy(
-                out=whhT[:, run * RUN * P : (run + 1) * RUN * P, :].rearrange("p n e -> p (n e)"),
+                out=whhT[:, half_n * BANK : (half_n + 1) * BANK, :].rearrange("p n e -> p (n e)"),
                 in_=whh_bank[:].rearrange("p i n -> p (i n)").bitcast(BF16),
             )
-        quantise(0)
-        transpose_hh(0)
 
         def spread_over_partitions(first, spread):
             for c in range(spread.shape[1] // P):
@@ -343,58 +351,76 @@ def tile_hyperlstmcell_pa_kernel(
                     ident_bf16[:],
                 )
 
+        transpose_u(0)
+        transpose_whh(0)
+        transpose_hh(0)
+        quantise(0)
+        plain_product(0, 0)
+        transpose_whh(1)
+        mx_product(0, 0)
+        join(0, 0)
+        plain_product(0, 1)
+        norm_cols_bank = work_psum.tile([P, P], BF16, tag="work")
+        nc.tensor.transpose(norm_cols_bank[:], norm_rows[:], ident_bf16[:])
+        norm_cols = keep.tile([P, 20], BF16)
+        nc.scalar.copy(out=norm_cols[:], in_=norm_cols_bank[:, 0:20])
+        mx_product(0, 1)
         to_spread = [(0, gamma_bc), (8, beta_bc), (16, c_norm_bc)]
         spread_over_partitions(*to_spread[0])
-        plain_product(0)
-        mx_product(0)
 
-        for r in range(BATCH_TILES + 2):
-            ahead, now, cell, last = r + 1, r, r - 1, r - 2
-            if live(ahead):
-                transpose_hh(ahead)
+        def squash_cell(t):
+            nc.scalar.activation(out=tanh_c[t][:], in_=new_c[t][:], func=ACT.Tanh)
+
+        for r in range(BATCH_TILES + 3):
+            ahead, now, summed, normed_c, last = r + 1, r, r - 1, r - 2, r - 3
             if live(now):
-                join(now)
+                join(now, 1)
                 std_plus_eps(scaled_sq[now][:], root[now][:], std[now][:])
             if live(ahead):
+                transpose_hh(ahead)
                 transpose_u(ahead)
-            if live(cell):
-                cell_products(cell)
+            if live(summed):
+                cell_products(summed)
             if live(now):
                 gate_mean(now)
-            if live(cell):
-                cell_sum(cell)
+            if live(normed_c):
+                centre_cell(normed_c)
+            if live(summed):
+                cell_sum(summed)
+                sum_of_squares(raw_c[summed][:], c_sum[summed][:], c_scaled_sq[summed][:])
+                std_plus_eps(c_scaled_sq[summed][:], c_root[summed][:], c_std[summed][:])
             if live(now):
                 for j in CELL_GATES:
                     centre_gate(now, j)
             if live(ahead):
                 quantise(ahead)
-            if live(last):
-                nc.scalar.activation(out=tanh_c[last][:], in_=new_c[last][:], func=ACT.Tanh)
-                hidden(last)
-            if live(cell):
-                squash_gate(cell, GATE_O)
-                sum_of_squares(raw_c[cell][:], c_sum[cell][:], c_scaled_sq[cell][:])
-                std_plus_eps(c_scaled_sq[cell][:], c_root[cell][:], c_std[cell][:])
-                cell_mean(cell)
+            if live(normed_c):
+                nc.vector.reciprocal(out=c_inv[normed_c][:], in_=c_std[normed_c][:])
+            if live(summed):
+                cell_mean(summed)
             if live(now):
                 centre_gate(now, GATE_O)
             if live(ahead):
-                plain_product(ahead)
+                for half_n in range(HALVES):
+                    plain_product(ahead, half_n)
             if ahead < len(to_spread):
                 spread_over_partitions(*to_spread[ahead])
             if live(ahead):
-                mx_product(ahead)
+                for half_n in range(HALVES):
+                    mx_product(ahead, half_n)
             if live(now):
                 nc.vector.reciprocal(out=inv[now][:], in_=std[now][:])
-            if live(cell):
-                centre_cell(cell)
+            if live(last):
+                hidden(last)
             if live(now):
                 for j in CELL_GATES:
                     norm_gate(now, j)
                     squash_gate(now, j)
-            if live(cell):
-                nc.vector.reciprocal(out=c_inv[cell][:], in_=c_std[cell][:])
+            if live(normed_c):
+                norm_cell(normed_c)
+                squash_cell(normed_c)
             if live(now):
                 norm_gate(now, GATE_O)
-            if live(cell):
-                norm_cell(cell)
+                squash_gate(now, GATE_O)
+            if live(ahead):
+                join(ahead, 0)

@@ -92,11 +92,13 @@ def tile_hyperlstmcell_pa_kernel(
         half = keep.tile([P, GATES], F32)
         nc.vector.memset(half[:], 0.5)
 
+        hh_sb = keep.tile([P, BATCH_TILES, UNITS], BF16)
+        nc.scalar.dma_start(out=hh_sb[:, 0, :], in_=hyper_h[batch_rows(0), :])
+        nc.scalar.dma_start(out=bias_row[0:1, :], in_=hc_bih.unsqueeze(0))
         warm = keep.tile([P, 1], F32)
         nc.scalar.activation(out=warm[:], in_=gate_shift[:, 0:1], func=ACT.Sigmoid)
 
         u_sb = per_tile("u_sb", [P, K], BF16)
-        hh_sb = keep.tile([P, BATCH_TILES, UNITS], BF16)
         hc_sb = keep.tile([P, BATCH_TILES, UNITS], BF16)
         whh_sb = keep.tile([P, N // P, UNITS], BF16)
         w_words = [
@@ -121,8 +123,11 @@ def tile_hyperlstmcell_pa_kernel(
                 in_=hc_Wih_words[:, :, some].bitcast(I32).rearrange("g p c -> p g c"),
             )
 
-        nc.gpsimd.dma_start(out=hh_sb[:], in_=hyper_h.rearrange("(t p) k -> p t k", p=P))
-        nc.gpsimd.dma_start(out=bias_row[0:1, :], in_=hc_bih.unsqueeze(0))
+        def load_hh(first, end):
+            nc.sync.dma_start(
+                out=hh_sb[:, first:end, :], in_=hyper_h[first * P : end * P, :].rearrange("(t p) k -> p t k", p=P)
+            )
+
         ident_f32 = keep.tile([P, P], F32)
         make_identity(nc, ident_f32[:])
         ident_bf16 = keep.tile([P, P], BF16)
@@ -141,7 +146,9 @@ def tile_hyperlstmcell_pa_kernel(
         nc.sync.dma_start(out=norm_rows[8:16, :], in_=hc_ln_beta.rearrange("g (c n) -> (g c) n", n=P))
         nc.sync.dma_start(out=norm_rows[16:18, :], in_=hc_lnc_gamma.rearrange("(c n) -> c n", n=P))
         nc.sync.dma_start(out=norm_rows[18:20, :], in_=hc_lnc_beta.rearrange("(c n) -> c n", n=P))
-        for t in range(1, BATCH_TILES):
+        load_u(1)
+        load_hh(1, BATCH_TILES)
+        for t in range(2, BATCH_TILES):
             load_u(t)
         nc.sync.dma_start(out=hc_sb[:], in_=hyper_c.rearrange("(t p) k -> p t k", p=P))
 

@@ -189,7 +189,10 @@ def tile_hyperlstmcell_pa_kernel(
         def transpose_hh(t):
             hh_bank = work_psum.tile([P, P], F32, tag="work")
             nc.tensor.transpose(hh_bank[:], hh_sb[:, t, :].bitcast(F32), ident_f32[:])
-            nc.scalar.copy(out=hhT[t][:].rearrange("p b e -> p (b e)"), in_=hh_bank[:].bitcast(BF16))
+            return hh_bank
+
+        def copy_hh(t, hh_bank, engine_copy):
+            engine_copy(out=hhT[t][:].rearrange("p b e -> p (b e)"), in_=hh_bank[:].bitcast(BF16))
 
         def transpose_u(t):
             u_words = u_sb[t][:].bitcast(F32)
@@ -294,9 +297,9 @@ def tile_hyperlstmcell_pa_kernel(
                 bias=gate_shift[:, j : j + 1],
             )
 
-        def cell_products(t):
-            nc.vector.tensor_tensor(out=kept[t][:], in0=hc_sb[:, t, :], in1=act[t][:, gate_cols(GATE_F)], op=ALU.mult)
-            nc.vector.tensor_tensor(
+        def cell_products(t, engine):
+            engine.tensor_tensor(out=kept[t][:], in0=hc_sb[:, t, :], in1=act[t][:, gate_cols(GATE_F)], op=ALU.mult)
+            engine.tensor_tensor(
                 out=written[t][:], in0=act[t][:, gate_cols(GATE_I)], in1=act[t][:, gate_cols(GATE_G)], op=ALU.mult
             )
 
@@ -335,8 +338,8 @@ def tile_hyperlstmcell_pa_kernel(
             )
             nc.sync.dma_start(out=out_1[batch_rows(t), :], in_=new_c[t][:])
 
-        def hidden(t):
-            nc.vector.tensor_tensor(out=new_h[t][:], in0=tanh_c[t][:], in1=act[t][:, gate_cols(GATE_O)], op=ALU.mult)
+        def hidden(t, engine):
+            engine.tensor_tensor(out=new_h[t][:], in0=tanh_c[t][:], in1=act[t][:, gate_cols(GATE_O)], op=ALU.mult)
             nc.sync.dma_start(out=out_0[batch_rows(t), :], in_=new_h[t][:])
 
         whh_words = whh_sb[:].bitcast(F32)
@@ -360,7 +363,7 @@ def tile_hyperlstmcell_pa_kernel(
 
         transpose_u(0)
         transpose_whh(0)
-        transpose_hh(0)
+        copy_hh(0, transpose_hh(0), nc.scalar.copy)
         quantise(0)
         plain_product(0, 0)
         transpose_whh(1)
@@ -380,14 +383,17 @@ def tile_hyperlstmcell_pa_kernel(
 
         for r in range(BATCH_TILES + 3):
             ahead, now, summed, normed_c, last = r + 1, r, r - 1, r - 2, r - 3
+            if live(ahead):
+                hh_bank = transpose_hh(ahead)
             if live(now):
                 join(now, 1)
                 std_plus_eps(scaled_sq[now][:], root[now][:], std[now][:])
             if live(ahead):
-                transpose_hh(ahead)
                 transpose_u(ahead)
-            if live(summed):
-                cell_products(summed)
+            if summed == BATCH_TILES - 1:
+                cell_products(summed, nc.vector)
+            if live(ahead):
+                copy_hh(ahead, hh_bank, nc.vector.tensor_copy)
             if live(now):
                 gate_mean(now)
             if live(normed_c):
@@ -396,6 +402,8 @@ def tile_hyperlstmcell_pa_kernel(
                 cell_sum(summed)
                 sum_of_squares(raw_c[summed][:], c_sum[summed][:], c_scaled_sq[summed][:])
                 std_plus_eps(c_scaled_sq[summed][:], c_root[summed][:], c_std[summed][:])
+            if live(last):
+                hidden(last, nc.gpsimd if live(now) else nc.vector)
             if live(now):
                 for j in CELL_GATES:
                     centre_gate(now, j)
@@ -405,8 +413,6 @@ def tile_hyperlstmcell_pa_kernel(
                 nc.vector.reciprocal(out=c_inv[normed_c][:], in_=c_std[normed_c][:])
             if live(summed):
                 cell_mean(summed)
-            if live(now):
-                centre_gate(now, GATE_O)
             if live(ahead):
                 for half_n in range(HALVES):
                     plain_product(ahead, half_n)
@@ -417,12 +423,12 @@ def tile_hyperlstmcell_pa_kernel(
                     mx_product(ahead, half_n)
             if live(now):
                 nc.vector.reciprocal(out=inv[now][:], in_=std[now][:])
-            if live(last):
-                hidden(last)
-            if live(now):
+                centre_gate(now, GATE_O)
                 for j in CELL_GATES:
                     norm_gate(now, j)
                     squash_gate(now, j)
+            if live(now) and live(ahead):
+                cell_products(now, nc.gpsimd)
             if live(normed_c):
                 norm_cell(normed_c)
                 squash_cell(normed_c)

@@ -82,7 +82,7 @@ def tile_hyperlstmcell_pa_kernel(
         nc.vector.memset(bias_row[:], 0.0)
         w_scales = keep.tile([P, PASSES, N], U8, align_bytes=64)
         nc.vector.memset(w_scales[:].bitcast(I32), 0)
-        norm_rows = keep.tile([P, P], BF16)
+        norm_rows = keep.tile([P, UNITS], BF16)
         nc.vector.memset(norm_rows[:], 0.0)
         gate_shift = keep.tile([P, GATES], F32)
         nc.vector.memset(gate_shift[:], 0.0)
@@ -130,22 +130,20 @@ def tile_hyperlstmcell_pa_kernel(
 
         ident_f32 = keep.tile([P, P], F32)
         make_identity(nc, ident_f32[:])
-        ident_bf16 = keep.tile([P, P], BF16)
-        make_identity(nc, ident_bf16[:])
         load_u(0)
         load_whh(0)
+        load_whh(1)
         for quad in range(4):
             nc.sync.dma_start(
                 out=w_scales[32 * quad : 32 * quad + 4, :, :].bitcast(I32),
                 in_=hc_Wih_scales[:, 4 * quad : 4 * quad + 4, :].bitcast(I32).rearrange("g r c -> r g c"),
             )
         load_w_words(0)
-        load_whh(1)
         load_w_words(1)
-        nc.sync.dma_start(out=norm_rows[0:8, :], in_=hc_ln_gamma.rearrange("g (c n) -> (g c) n", n=P))
-        nc.sync.dma_start(out=norm_rows[8:16, :], in_=hc_ln_beta.rearrange("g (c n) -> (g c) n", n=P))
-        nc.sync.dma_start(out=norm_rows[16:18, :], in_=hc_lnc_gamma.rearrange("(c n) -> c n", n=P))
-        nc.sync.dma_start(out=norm_rows[18:20, :], in_=hc_lnc_beta.rearrange("(c n) -> c n", n=P))
+        nc.sync.dma_start(out=norm_rows[0:GATES, :], in_=hc_ln_gamma)
+        nc.sync.dma_start(out=norm_rows[GATES : 2 * GATES, :], in_=hc_ln_beta)
+        nc.sync.dma_start(out=norm_rows[2 * GATES : 2 * GATES + 1, :], in_=hc_lnc_gamma.unsqueeze(0))
+        nc.sync.dma_start(out=norm_rows[2 * GATES + 1 : 2 * GATES + 2, :], in_=hc_lnc_beta.unsqueeze(0))
         load_u(1)
         load_hh(1, BATCH_TILES)
         for t in range(2, BATCH_TILES):
@@ -354,28 +352,29 @@ def tile_hyperlstmcell_pa_kernel(
             )
 
         def spread_over_partitions(first, spread):
-            for c in range(spread.shape[1] // P):
+            spread_words = spread[:].bitcast(F32)
+            for c in range(spread_words.shape[1] // P):
                 nc.tensor.transpose(
-                    spread[:, c * P : (c + 1) * P],
+                    spread_words[:, c * P : (c + 1) * P],
                     norm_cols[:, first + c : first + c + 1].to_broadcast([P, P]),
-                    ident_bf16[:],
+                    ident_f32[:],
                 )
 
         transpose_u(0)
         transpose_whh(0)
+        transpose_whh(1)
         copy_hh(0, transpose_hh(0), nc.scalar.copy)
         quantise(0)
         plain_product(0, 0)
-        transpose_whh(1)
+        plain_product(0, 1)
         mx_product(0, 0)
         join(0, 0)
-        plain_product(0, 1)
-        norm_cols_bank = work_psum.tile([P, P], BF16, tag="work")
-        nc.tensor.transpose(norm_cols_bank[:], norm_rows[:], ident_bf16[:])
-        norm_cols = keep.tile([P, 20], BF16)
-        nc.scalar.copy(out=norm_cols[:], in_=norm_cols_bank[:, 0:20])
         mx_product(0, 1)
-        to_spread = [(0, gamma_bc), (8, beta_bc), (16, c_norm_bc)]
+        norm_cols_bank = work_psum.tile([P, P], F32, tag="work")
+        nc.tensor.transpose(norm_cols_bank[:], norm_rows[:].bitcast(F32), ident_f32[:])
+        norm_cols = keep.tile([P, 2 * GATES + 2], F32)
+        nc.scalar.copy(out=norm_cols[:], in_=norm_cols_bank[:, 0 : 2 * GATES + 2])
+        to_spread = [(0, gamma_bc), (GATES, beta_bc), (2 * GATES, c_norm_bc)]
         spread_over_partitions(*to_spread[0])
 
         def squash_cell(t):

@@ -380,29 +380,41 @@ def tile_hyperlstmcell_pa_kernel(
         def squash_cell(t):
             nc.scalar.activation(out=tanh_c[t][:], in_=new_c[t][:], func=ACT.Tanh)
 
+        def by_bank(t):
+            return t == BATCH_TILES - 1
+
+        def bank_gates(half_n):
+            return slice(half_n * GATES_PER_BANK, (half_n + 1) * GATES_PER_BANK)
+
+        def gate_std(t, gates):
+            std_plus_eps(scaled_sq[t][:, gates], root[t][:, gates], std[t][:, gates])
+
+        def gate_inv(t, gates):
+            nc.vector.reciprocal(out=inv[t][:, gates], in_=std[t][:, gates])
+
         for r in range(BATCH_TILES + 3):
             ahead, now, summed, normed_c, last = r + 1, r, r - 1, r - 2, r - 3
             if live(ahead):
                 hh_bank = transpose_hh(ahead)
             if live(now):
                 join(now, 1)
-                std_plus_eps(scaled_sq[now][:], root[now][:], std[now][:])
+                gate_std(now, bank_gates(1) if by_bank(now) else slice(0, GATES))
             if live(ahead):
                 transpose_u(ahead)
             if summed == BATCH_TILES - 1:
                 cell_products(summed, nc.vector)
             if live(ahead):
                 copy_hh(ahead, hh_bank, nc.vector.tensor_copy)
-            if live(now):
-                gate_mean(now)
             if live(normed_c):
                 centre_cell(normed_c)
+            if live(now):
+                gate_mean(now)
+            if live(last):
+                hidden(last, nc.gpsimd if last < BATCH_TILES // 2 else nc.vector)
             if live(summed):
                 cell_sum(summed)
                 sum_of_squares(raw_c[summed][:], c_sum[summed][:], c_scaled_sq[summed][:])
                 std_plus_eps(c_scaled_sq[summed][:], c_root[summed][:], c_std[summed][:])
-            if live(last):
-                hidden(last, nc.gpsimd if live(now) else nc.vector)
             if live(now):
                 for j in CELL_GATES:
                     centre_gate(now, j)
@@ -421,9 +433,11 @@ def tile_hyperlstmcell_pa_kernel(
                 for half_n in range(HALVES):
                     mx_product(ahead, half_n)
             if live(now):
-                nc.vector.reciprocal(out=inv[now][:], in_=std[now][:])
+                gate_inv(now, bank_gates(0) if by_bank(now) else slice(0, GATES))
                 centre_gate(now, GATE_O)
                 for j in CELL_GATES:
+                    if by_bank(now) and j == GATE_G:
+                        gate_inv(now, bank_gates(1))
                     norm_gate(now, j)
                     squash_gate(now, j)
             if live(now) and live(ahead):
@@ -436,3 +450,5 @@ def tile_hyperlstmcell_pa_kernel(
                 squash_gate(now, GATE_O)
             if live(ahead):
                 join(ahead, 0)
+                if by_bank(ahead):
+                    gate_std(ahead, bank_gates(0))

@@ -132,13 +132,13 @@ def tile_hyperlstmcell_pa_kernel(
         make_identity(nc, ident_f32[:])
         load_u(0)
         load_whh(0)
-        load_whh(1)
+        load_w_words(0)
         for quad in range(4):
             nc.sync.dma_start(
                 out=w_scales[32 * quad : 32 * quad + 4, :, :].bitcast(I32),
                 in_=hc_Wih_scales[:, 4 * quad : 4 * quad + 4, :].bitcast(I32).rearrange("g r c -> r g c"),
             )
-        load_w_words(0)
+        load_whh(1)
         load_w_words(1)
         nc.sync.dma_start(out=norm_rows[0:GATES, :], in_=hc_ln_gamma)
         nc.sync.dma_start(out=norm_rows[GATES : 2 * GATES, :], in_=hc_ln_beta)
@@ -362,18 +362,18 @@ def tile_hyperlstmcell_pa_kernel(
 
         transpose_u(0)
         transpose_whh(0)
-        transpose_whh(1)
         copy_hh(0, transpose_hh(0), nc.scalar.copy)
         quantise(0)
         plain_product(0, 0)
-        plain_product(0, 1)
+        transpose_whh(1)
         mx_product(0, 0)
         join(0, 0)
-        mx_product(0, 1)
+        plain_product(0, 1)
         norm_cols_bank = work_psum.tile([P, P], F32, tag="work")
         nc.tensor.transpose(norm_cols_bank[:], norm_rows[:].bitcast(F32), ident_f32[:])
         norm_cols = keep.tile([P, 2 * GATES + 2], F32)
         nc.scalar.copy(out=norm_cols[:], in_=norm_cols_bank[:, 0 : 2 * GATES + 2])
+        mx_product(0, 1)
         to_spread = [(0, gamma_bc), (GATES, beta_bc), (2 * GATES, c_norm_bc)]
         spread_over_partitions(*to_spread[0])
 

@@ -78,15 +78,34 @@ def tile_hyperlstmcell_pa_kernel(
                 keep.tile(shape, dtype, name="%s%d" % (name, t), align_bytes=align_bytes) for t in range(BATCH_TILES)
             ]
 
+        idle_in = keep.tile([P, K_PASS], BF16, align_bytes=64)
+        nc.gpsimd.memset(idle_in[:].bitcast(I32), 0)
+        w_words = [
+            keep.tile(
+                [P, PASSES + (half_n == HALVES - 1), 2 * BANK], U8, name="w_words%d" % half_n, align_bytes=64
+            )
+            for half_n in range(HALVES)
+        ]
+        w_scales = keep.tile([P, PASSES + 1, N], U8, align_bytes=64)
+        idle_words = w_words[HALVES - 1][:, PASSES, :]
+        idle_scales = w_scales[:, PASSES, 0:BANK]
         bias_row = keep.tile([P, N], BF16)
-        nc.vector.memset(bias_row[:], 0.0)
-        w_scales = keep.tile([P, PASSES, N], U8, align_bytes=64)
-        nc.vector.memset(w_scales[:].bitcast(I32), 0)
-        norm_rows = keep.tile([P, UNITS], BF16)
-        nc.vector.memset(norm_rows[:], 0.0)
+        nc.gpsimd.memset(bias_row[:].bitcast(I32), 0)
+        ident_f32 = keep.tile([P, P], F32)
+        make_identity(nc, ident_f32[:])
         gate_shift = keep.tile([P, GATES], F32)
         nc.vector.memset(gate_shift[:], 0.0)
         nc.vector.memset(gate_shift[:, GATE_F : GATE_F + 1], 1.0)
+        idle_codes = keep.tile([P, P], U32, align_bytes=64)
+        idle_code_scales = keep.tile([P, P], U8, align_bytes=64)
+        nc.vector.quantize_mx(
+            out=idle_codes[:].bitcast(FP8X4), scales=idle_code_scales[:], in_=idle_in[:]
+        )
+        nc.vector.memset(idle_words.bitcast(I32), 0)
+        nc.vector.memset(idle_scales.bitcast(I32), 0)
+        nc.vector.memset(w_scales[:, 0:PASSES, :].bitcast(I32), 0)
+        norm_rows = keep.tile([P, UNITS], BF16)
+        nc.vector.memset(norm_rows[:].bitcast(I32), 0)
         ones = keep.tile([P, P], BF16)
         nc.vector.memset(ones[:], 1.0)
         half = keep.tile([P, GATES], F32)
@@ -101,9 +120,6 @@ def tile_hyperlstmcell_pa_kernel(
         u_sb = per_tile("u_sb", [P, K], BF16)
         hc_sb = keep.tile([P, BATCH_TILES, UNITS], BF16)
         whh_sb = keep.tile([P, N // P, UNITS], BF16)
-        w_words = [
-            keep.tile([P, PASSES, 2 * BANK], U8, name="w_words%d" % half_n, align_bytes=64) for half_n in range(HALVES)
-        ]
 
         def load_u(t):
             nc.sync.dma_start(out=u_sb[t][:, 0:IN], in_=x[batch_rows(t), :])
@@ -119,7 +135,7 @@ def tile_hyperlstmcell_pa_kernel(
         def load_w_words(half_n):
             some = slice(2 * half_n * BANK, 2 * (half_n + 1) * BANK)
             nc.sync.dma_start(
-                out=w_words[half_n][:].bitcast(I32),
+                out=w_words[half_n][:, 0:PASSES, :].bitcast(I32),
                 in_=hc_Wih_words[:, :, some].bitcast(I32).rearrange("g p c -> p g c"),
             )
 
@@ -128,14 +144,12 @@ def tile_hyperlstmcell_pa_kernel(
                 out=hh_sb[:, first:end, :], in_=hyper_h[first * P : end * P, :].rearrange("(t p) k -> p t k", p=P)
             )
 
-        ident_f32 = keep.tile([P, P], F32)
-        make_identity(nc, ident_f32[:])
-        load_u(0)
         load_whh(0)
+        load_u(0)
         load_w_words(0)
         for quad in range(4):
             nc.sync.dma_start(
-                out=w_scales[32 * quad : 32 * quad + 4, :, :].bitcast(I32),
+                out=w_scales[32 * quad : 32 * quad + 4, 0:PASSES, :].bitcast(I32),
                 in_=hc_Wih_scales[:, 4 * quad : 4 * quad + 4, :].bitcast(I32).rearrange("g r c -> r g c"),
             )
         load_whh(1)
@@ -144,8 +158,8 @@ def tile_hyperlstmcell_pa_kernel(
         nc.sync.dma_start(out=norm_rows[GATES : 2 * GATES, :], in_=hc_ln_beta)
         nc.sync.dma_start(out=norm_rows[2 * GATES : 2 * GATES + 1, :], in_=hc_lnc_gamma.unsqueeze(0))
         nc.sync.dma_start(out=norm_rows[2 * GATES + 1 : 2 * GATES + 2, :], in_=hc_lnc_beta.unsqueeze(0))
-        load_u(1)
         load_hh(1, BATCH_TILES)
+        load_u(1)
         for t in range(2, BATCH_TILES):
             load_u(t)
         nc.sync.dma_start(out=hc_sb[:], in_=hyper_c.rearrange("(t p) k -> p t k", p=P))
@@ -154,6 +168,11 @@ def tile_hyperlstmcell_pa_kernel(
         gamma_bc = const_psum.tile([P, N], BF16)
         beta_bc = const_psum.tile([P, N], BF16)
         c_norm_bc = const_psum.tile([P, 2 * UNITS], BF16)
+        o_cols = keep.tile([P, 2, 2], F32)
+        scaled_mean = per_tile("scaled_mean", [P, 1], F32)
+        z_o = per_tile("z_o", [P, 2, P], F32)
+        o_units = [keep.tile([P, 2, 2, P], F32, name="o_units%d" % k) for k in range(2)]
+        o_banks = [None, None]
         hhT = per_tile("hhT", [P, P, K_PLAIN], BF16)
         grouped = per_tile("grouped", [P, PASSES, P, 4], BF16, align_bytes=64)
         u_codes = per_tile("u_codes", [P, PASSES * P], U32, align_bytes=64)
@@ -184,13 +203,14 @@ def tile_hyperlstmcell_pa_kernel(
         tanh_c = per_tile("tanh_c", [P, UNITS], F32)
         new_h = per_tile("new_h", [P, UNITS], F32)
 
-        def transpose_hh(t):
-            hh_bank = work_psum.tile([P, P], F32, tag="work")
-            nc.tensor.transpose(hh_bank[:], hh_sb[:, t, :].bitcast(F32), ident_f32[:])
+        def transpose_hh(t, hh_bank=None):
+            if hh_bank is None:
+                hh_bank = work_psum.tile([P, P], F32, tag="work")
+            nc.tensor.transpose(hh_bank[:, 0:P], hh_sb[:, t, :].bitcast(F32), ident_f32[:])
             return hh_bank
 
         def copy_hh(t, hh_bank, engine_copy):
-            engine_copy(out=hhT[t][:].rearrange("p b e -> p (b e)"), in_=hh_bank[:].bitcast(BF16))
+            engine_copy(out=hhT[t][:].rearrange("p b e -> p (b e)"), in_=hh_bank[:, 0:P].bitcast(BF16))
 
         def transpose_u(t):
             u_words = u_sb[t][:].bitcast(F32)
@@ -223,9 +243,13 @@ def tile_hyperlstmcell_pa_kernel(
             nc.tensor.matmul(acc[:], lhsT=ones[:], rhs=bias_row[:, cols], start=False, stop=True)
             nc.scalar.copy(out=plain[t][:, cols], in_=acc[:])
 
+        def take_mx_bank(t):
+            mx_banks[t].append(mx_psum.tile([P, BANK], F32, tag="mx", name="mx_acc"))
+
         def mx_product(t, half_n):
-            bank = mx_psum.tile([P, BANK], F32, tag="mx", name="mx_acc")
-            mx_banks[t].append(bank)
+            if len(mx_banks[t]) == half_n:
+                take_mx_bank(t)
+            bank = mx_banks[t][half_n]
             for g in range(PASSES):
                 rows = slice(g * P, (g + 1) * P)
                 nc.tensor.matmul_mx(
@@ -253,6 +277,10 @@ def tile_hyperlstmcell_pa_kernel(
 
         def join(t, half_n):
             for j in range(half_n * GATES_PER_BANK, (half_n + 1) * GATES_PER_BANK):
+                join_gate(t, j)
+
+        def join_gate(t, j):
+                half_n = j // GATES_PER_BANK
                 nc.vector.scalar_tensor_tensor(
                     out=v[t][:, gate_cols(j)],
                     in0=mx_banks[t][half_n][:, gate_cols(j % GATES_PER_BANK)],
@@ -295,11 +323,44 @@ def tile_hyperlstmcell_pa_kernel(
                 bias=gate_shift[:, j : j + 1],
             )
 
-        def cell_products(t, engine):
+        def o_shift(t):
+            one = slice(GATE_O, GATE_O + 1)
+            nc.vector.tensor_tensor(out=scaled_mean[t][:], in0=neg_mean[t][:, one], in1=inv[t][:, one], op=ALU.mult)
+
+        def o_z(t):
+            one = slice(GATE_O, GATE_O + 1)
+            nc.scalar.activation(out=z_o[t][:], in_=v[t][:, gate_cols(GATE_O)].rearrange("p (q e) -> p e q", e=2), func=ACT.Identity, scale=inv[t][:, one], bias=scaled_mean[t][:])
+
+        def o_squash(k):
+            bank = work_psum.tile([P, 2, 2, P], F32, tag="work")
+            for i in range(2):
+                for e in range(2):
+                    nc.tensor.transpose(bank[:, e, i, :], z_o[2 * k + i][:, e, :], ident_f32[:])
+            for e in range(2):
+                nc.scalar.activation(out=o_units[k][:, e, :, :], in_=bank[:, e, :, :], func=ACT.Sigmoid, scale=o_cols[:, 0, e : e + 1], bias=o_cols[:, 1, e : e + 1])
+
+        def o_back(k):
+            bank = work_psum.tile([P, 2, 2, P], F32, tag="work")
+            for i in range(2):
+                for e in range(2):
+                    nc.tensor.transpose(bank[:, i, e, :], o_units[k][:, e, i, :], ident_f32[:])
+            o_banks[k] = bank
+
+        def hidden_o(t):
+            nc.vector.tensor_tensor(out=new_h[t][:].rearrange("p (q e) -> p q e", e=2), in0=tanh_c[t][:].rearrange("p (q e) -> p q e", e=2), in1=o_banks[t // 2][:, t % 2, :, :].rearrange("p e q -> p q e"), op=ALU.mult)
+            nc.sync.dma_start(out=out_0[batch_rows(t), :], in_=new_h[t][:])
+
+        def kept_product(t, engine):
             engine.tensor_tensor(out=kept[t][:], in0=hc_sb[:, t, :], in1=act[t][:, gate_cols(GATE_F)], op=ALU.mult)
+
+        def written_product(t, engine):
             engine.tensor_tensor(
                 out=written[t][:], in0=act[t][:, gate_cols(GATE_I)], in1=act[t][:, gate_cols(GATE_G)], op=ALU.mult
             )
+
+        def cell_products(t, engine):
+            kept_product(t, engine)
+            written_product(t, engine)
 
         def cell_sum(t):
             nc.vector.scalar_tensor_tensor(
@@ -353,29 +414,51 @@ def tile_hyperlstmcell_pa_kernel(
 
         def spread_over_partitions(first, spread):
             spread_words = spread[:].bitcast(F32)
-            for c in range(spread_words.shape[1] // P):
+            for c in range(min(3, spread_words.shape[1] // P)):
                 nc.tensor.transpose(
                     spread_words[:, c * P : (c + 1) * P],
                     norm_cols[:, first + c : first + c + 1].to_broadcast([P, P]),
                     ident_f32[:],
                 )
 
-        transpose_u(0)
+        def warm_up(passes):
+            for i in range(passes):
+                nc.tensor.matmul_mx(
+                    out=mx_banks[0][0][:],
+                    lhsT=idle_codes[:].bitcast(FP8X4),
+                    lhsT_scale=idle_code_scales[:],
+                    rhs=idle_words.bitcast(FP4X4),
+                    rhs_scale=idle_scales,
+                    start=True,
+                    stop=True,
+                )
+
+        take_mx_bank(0)
+        take_mx_bank(0)
+        warm_up(2)
         transpose_whh(0)
-        copy_hh(0, transpose_hh(0), nc.scalar.copy)
-        quantise(0)
+        copy_hh(0, transpose_hh(0, mx_banks[0][1]), nc.vector.tensor_copy)
+        transpose_u(0)
+        warm_up(0)
+        for pair in range(PASSES // 2):
+            some = slice(pair * 2 * P, (pair + 1) * 2 * P)
+            nc.vector.quantize_mx(
+                out=u_codes[0][:, some].bitcast(FP8X4),
+                scales=u_scales[0][:, some],
+                in_=grouped[0][:, 2 * pair : 2 * pair + 2, :, :].rearrange("p g b j -> p (g b j)"),
+            )
         plain_product(0, 0)
         transpose_whh(1)
         mx_product(0, 0)
-        join(0, 0)
         plain_product(0, 1)
+        join(0, 0)
+        mx_product(0, 1)
         norm_cols_bank = work_psum.tile([P, P], F32, tag="work")
         nc.tensor.transpose(norm_cols_bank[:], norm_rows[:].bitcast(F32), ident_f32[:])
         norm_cols = keep.tile([P, 2 * GATES + 2], F32)
-        nc.scalar.copy(out=norm_cols[:], in_=norm_cols_bank[:, 0 : 2 * GATES + 2])
-        mx_product(0, 1)
+        nc.vector.tensor_copy(out=norm_cols[:], in_=norm_cols_bank[:, 0 : 2 * GATES + 2])
+        copy_hh(1, transpose_hh(1), nc.vector.tensor_copy)
         to_spread = [(0, gamma_bc), (GATES, beta_bc), (2 * GATES, c_norm_bc)]
-        spread_over_partitions(*to_spread[0])
 
         def squash_cell(t):
             nc.scalar.activation(out=tanh_c[t][:], in_=new_c[t][:], func=ACT.Tanh)
@@ -392,63 +475,118 @@ def tile_hyperlstmcell_pa_kernel(
         def gate_inv(t, gates):
             nc.vector.reciprocal(out=inv[t][:, gates], in_=std[t][:, gates])
 
-        for r in range(BATCH_TILES + 3):
-            ahead, now, summed, normed_c, last = r + 1, r, r - 1, r - 2, r - 3
-            if live(ahead):
-                hh_bank = transpose_hh(ahead)
-            if live(now):
-                join(now, 1)
-                gate_std(now, bank_gates(1) if by_bank(now) else slice(0, GATES))
-            if live(ahead):
-                transpose_u(ahead)
-            if summed == BATCH_TILES - 1:
-                cell_products(summed, nc.vector)
-            if live(ahead):
-                copy_hh(ahead, hh_bank, nc.vector.tensor_copy)
-            if live(normed_c):
-                centre_cell(normed_c)
-            if live(now):
-                gate_mean(now)
-            if live(last):
-                hidden(last, nc.gpsimd if last < BATCH_TILES // 2 else nc.vector)
-            if live(summed):
-                cell_sum(summed)
-                sum_of_squares(raw_c[summed][:], c_sum[summed][:], c_scaled_sq[summed][:])
-                std_plus_eps(c_scaled_sq[summed][:], c_root[summed][:], c_std[summed][:])
-            if live(now):
-                for j in CELL_GATES:
-                    centre_gate(now, j)
-            if live(ahead):
-                quantise(ahead)
-            if live(normed_c):
-                nc.vector.reciprocal(out=c_inv[normed_c][:], in_=c_std[normed_c][:])
-            if live(summed):
-                cell_mean(summed)
-            if live(ahead):
-                for half_n in range(HALVES):
-                    plain_product(ahead, half_n)
-            if ahead < len(to_spread):
-                spread_over_partitions(*to_spread[ahead])
-            if live(ahead):
-                for half_n in range(HALVES):
-                    mx_product(ahead, half_n)
-            if live(now):
-                gate_inv(now, bank_gates(0) if by_bank(now) else slice(0, GATES))
-                centre_gate(now, GATE_O)
-                for j in CELL_GATES:
-                    if by_bank(now) and j == GATE_G:
-                        gate_inv(now, bank_gates(1))
-                    norm_gate(now, j)
-                    squash_gate(now, j)
-            if live(now) and live(ahead):
-                cell_products(now, nc.gpsimd)
-            if live(normed_c):
-                norm_cell(normed_c)
-                squash_cell(normed_c)
-            if live(now):
-                norm_gate(now, GATE_O)
-                squash_gate(now, GATE_O)
-            if live(ahead):
-                join(ahead, 0)
-                if by_bank(ahead):
-                    gate_std(ahead, bank_gates(0))
+        def gates(a, b):
+            return slice(a, b)
+
+        LOW, HIGH, ALL = slice(0, 2), slice(2, 4), slice(0, 4)
+        last = BATCH_TILES - 1
+
+        def mean_of(t, some):
+            nc.vector.tensor_scalar_mul(out=neg_mean[t][:, some], in0=sums[t][:, some], scalar1=-1.0 / UNITS)
+
+        def cell_stats(t):
+            cell_sum(t)
+            sum_of_squares(raw_c[t][:], c_sum[t][:], c_scaled_sq[t][:])
+            std_plus_eps(c_scaled_sq[t][:], c_root[t][:], c_std[t][:])
+
+        def cell_inv(t):
+            nc.vector.reciprocal(out=c_inv[t][:], in_=c_std[t][:])
+
+        def cell_finish(t):
+            norm_cell(t)
+            squash_cell(t)
+
+        def finish(t, j):
+            norm_gate(t, j)
+            squash_gate(t, j)
+
+        mean_of(0, LOW)
+        transpose_u(1)
+        join(0, 1)
+        gate_std(0, ALL)
+        spread_over_partitions(*to_spread[0])
+        plain_product(1, 0)
+        plain_product(1, 1)
+        centre_gate(0, GATE_F)
+        quantise(1)
+        mean_of(0, HIGH)
+        centre_gate(0, GATE_I)
+        centre_gate(0, GATE_G)
+        for k in range(2):
+            nc.vector.tensor_copy(out=o_cols[:, k, :], in_=norm_cols[:, k * GATES + GATE_O : k * GATES + GATE_O + 1].bitcast(BF16))
+        for n in range(1, BATCH_TILES):
+            prev, nxt, far = n - 1, n + 1, n + 2
+            mx_product(n, 0)
+            if live(nxt):
+                transpose_u(nxt)
+                hh_bank = transpose_hh(nxt)
+            if n < len(to_spread):
+                spread_over_partitions(*to_spread[n])
+            mx_product(n, 1)
+            join_gate(n, GATE_I)
+            if n >= 2:
+                cell_mean(n - 2)
+            join_gate(n, GATE_F)
+            if n == last:
+                gate_std(n, LOW)
+            else:
+                copy_hh(nxt, hh_bank, nc.vector.tensor_copy)
+            gate_inv(prev, ALL)
+            if n >= 2:
+                centre_cell(n - 2)
+            finish(prev, GATE_F)
+            finish(prev, GATE_I)
+            finish(prev, GATE_G)
+            o_shift(prev)
+            if n < last:
+                cell_products(prev, nc.gpsimd)
+            join(n, 1)
+            gate_std(n, HIGH if n == last else ALL)
+            mean_of(n, LOW)
+            if n < last:
+                plain_product(nxt, 0)
+                plain_product(nxt, 1)
+                quantise(nxt)
+            if n == last:
+                cell_products(2, nc.vector)
+            mean_of(n, HIGH)
+            centre_gate(n, GATE_F)
+            centre_gate(n, GATE_I)
+            if n == last:
+                cell_inv(0)
+                cell_inv(1)
+                gate_inv(n, LOW)
+            centre_gate(n, GATE_G)
+            if n < last:
+                cell_stats(prev)
+                pass
+        for t in range(last):
+            o_z(t)
+        o_squash(0)
+        finish(last, GATE_F)
+        gate_inv(last, HIGH)
+        finish(last, GATE_I)
+        finish(last, GATE_G)
+        o_shift(last)
+        cell_stats(2)
+        o_z(last)
+        kept_product(last, nc.vector)
+        o_back(0)
+        cell_mean(2)
+        cell_finish(0)
+        written_product(last, nc.vector)
+        cell_stats(last)
+        cell_finish(1)
+        o_squash(1)
+        centre_cell(2)
+        cell_inv(2)
+        cell_mean(last)
+        hidden_o(0)
+        cell_finish(2)
+        centre_cell(last)
+        o_back(1)
+        hidden_o(1)
+        cell_inv(last)
+        cell_finish(last)
+        hidden_o(2)
+        hidden_o(last)

@@ -78,32 +78,15 @@ def tile_hyperlstmcell_pa_kernel(
                 keep.tile(shape, dtype, name="%s%d" % (name, t), align_bytes=align_bytes) for t in range(BATCH_TILES)
             ]
 
-        idle_in = keep.tile([P, K_PASS], BF16, align_bytes=64)
-        nc.gpsimd.memset(idle_in[:].bitcast(I32), 0)
-        w_words = [
-            keep.tile(
-                [P, PASSES + (half_n == HALVES - 1), 2 * BANK], U8, name="w_words%d" % half_n, align_bytes=64
-            )
-            for half_n in range(HALVES)
-        ]
-        w_scales = keep.tile([P, PASSES + 1, N], U8, align_bytes=64)
-        idle_words = w_words[HALVES - 1][:, PASSES, :]
-        idle_scales = w_scales[:, PASSES, 0:BANK]
         bias_row = keep.tile([P, N], BF16)
         nc.gpsimd.memset(bias_row[:].bitcast(I32), 0)
+        w_scales = keep.tile([P, PASSES, N], U8, align_bytes=64)
+        nc.vector.memset(w_scales[:].bitcast(I32), 0)
         ident_f32 = keep.tile([P, P], F32)
         make_identity(nc, ident_f32[:])
         gate_shift = keep.tile([P, GATES], F32)
         nc.vector.memset(gate_shift[:], 0.0)
         nc.vector.memset(gate_shift[:, GATE_F : GATE_F + 1], 1.0)
-        idle_codes = keep.tile([P, P], U32, align_bytes=64)
-        idle_code_scales = keep.tile([P, P], U8, align_bytes=64)
-        nc.vector.quantize_mx(
-            out=idle_codes[:].bitcast(FP8X4), scales=idle_code_scales[:], in_=idle_in[:]
-        )
-        nc.vector.memset(idle_words.bitcast(I32), 0)
-        nc.vector.memset(idle_scales.bitcast(I32), 0)
-        nc.vector.memset(w_scales[:, 0:PASSES, :].bitcast(I32), 0)
         norm_rows = keep.tile([P, UNITS], BF16)
         nc.vector.memset(norm_rows[:].bitcast(I32), 0)
         ones = keep.tile([P, P], BF16)
@@ -120,6 +103,9 @@ def tile_hyperlstmcell_pa_kernel(
         u_sb = per_tile("u_sb", [P, K], BF16)
         hc_sb = keep.tile([P, BATCH_TILES, UNITS], BF16)
         whh_sb = keep.tile([P, N // P, UNITS], BF16)
+        w_words = [
+            keep.tile([P, PASSES, 2 * BANK], U8, name="w_words%d" % half_n, align_bytes=64) for half_n in range(HALVES)
+        ]
 
         def load_u(t):
             nc.sync.dma_start(out=u_sb[t][:, 0:IN], in_=x[batch_rows(t), :])
@@ -135,7 +121,7 @@ def tile_hyperlstmcell_pa_kernel(
         def load_w_words(half_n):
             some = slice(2 * half_n * BANK, 2 * (half_n + 1) * BANK)
             nc.sync.dma_start(
-                out=w_words[half_n][:, 0:PASSES, :].bitcast(I32),
+                out=w_words[half_n][:].bitcast(I32),
                 in_=hc_Wih_words[:, :, some].bitcast(I32).rearrange("g p c -> p g c"),
             )
 
@@ -149,7 +135,7 @@ def tile_hyperlstmcell_pa_kernel(
         load_w_words(0)
         for quad in range(4):
             nc.sync.dma_start(
-                out=w_scales[32 * quad : 32 * quad + 4, 0:PASSES, :].bitcast(I32),
+                out=w_scales[32 * quad : 32 * quad + 4, :, :].bitcast(I32),
                 in_=hc_Wih_scales[:, 4 * quad : 4 * quad + 4, :].bitcast(I32).rearrange("g r c -> r g c"),
             )
         load_whh(1)
@@ -323,9 +309,14 @@ def tile_hyperlstmcell_pa_kernel(
                 bias=gate_shift[:, j : j + 1],
             )
 
+        unit = gamma_bc[:, gate_cols(GATE_O)]
+
+        def tiny(out, in_, factor):
+            nc.vector.scalar_tensor_tensor(out=out, in0=in_, scalar=factor, in1=unit[:, 0 : out.shape[1]], op0=ALU.mult, op1=ALU.mult)
+
         def o_shift(t):
             one = slice(GATE_O, GATE_O + 1)
-            nc.vector.tensor_tensor(out=scaled_mean[t][:], in0=neg_mean[t][:, one], in1=inv[t][:, one], op=ALU.mult)
+            tiny(scaled_mean[t][:], neg_mean[t][:, one], inv[t][:, one])
 
         def o_z(t):
             one = slice(GATE_O, GATE_O + 1)
@@ -374,7 +365,7 @@ def tile_hyperlstmcell_pa_kernel(
             )
 
         def cell_mean(t):
-            nc.vector.tensor_scalar_mul(out=c_neg_mean[t][:], in0=c_sum[t][:], scalar1=-1.0 / UNITS)
+            tiny(c_neg_mean[t][:], c_sum[t][:], -1.0 / UNITS)
 
         def centre_cell(t):
             nc.vector.scalar_tensor_tensor(
@@ -421,25 +412,14 @@ def tile_hyperlstmcell_pa_kernel(
                     ident_f32[:],
                 )
 
-        def warm_up(passes):
-            for i in range(passes):
-                nc.tensor.matmul_mx(
-                    out=mx_banks[0][0][:],
-                    lhsT=idle_codes[:].bitcast(FP8X4),
-                    lhsT_scale=idle_code_scales[:],
-                    rhs=idle_words.bitcast(FP4X4),
-                    rhs_scale=idle_scales,
-                    start=True,
-                    stop=True,
-                )
+        def spread_ones():
+            nc.tensor.transpose(gamma_bc[:].bitcast(F32)[:, 3 * P : 4 * P], ones[:].bitcast(F32)[:, 0:1].to_broadcast([P, P]), ident_f32[:])
 
         take_mx_bank(0)
         take_mx_bank(0)
-        warm_up(2)
         transpose_whh(0)
         copy_hh(0, transpose_hh(0, mx_banks[0][1]), nc.vector.tensor_copy)
         transpose_u(0)
-        warm_up(0)
         for pair in range(PASSES // 2):
             some = slice(pair * 2 * P, (pair + 1) * 2 * P)
             nc.vector.quantize_mx(
@@ -482,10 +462,9 @@ def tile_hyperlstmcell_pa_kernel(
         last = BATCH_TILES - 1
 
         def mean_of(t, some):
-            nc.vector.tensor_scalar_mul(out=neg_mean[t][:, some], in0=sums[t][:, some], scalar1=-1.0 / UNITS)
+            tiny(neg_mean[t][:, some], sums[t][:, some], -1.0 / UNITS)
 
-        def cell_stats(t):
-            cell_sum(t)
+        def cell_spread(t):
             sum_of_squares(raw_c[t][:], c_sum[t][:], c_scaled_sq[t][:])
             std_plus_eps(c_scaled_sq[t][:], c_root[t][:], c_std[t][:])
 
@@ -500,11 +479,12 @@ def tile_hyperlstmcell_pa_kernel(
             norm_gate(t, j)
             squash_gate(t, j)
 
-        mean_of(0, LOW)
         transpose_u(1)
+        spread_ones()
+        spread_over_partitions(*to_spread[0])
         join(0, 1)
         gate_std(0, ALL)
-        spread_over_partitions(*to_spread[0])
+        mean_of(0, LOW)
         plain_product(1, 0)
         plain_product(1, 1)
         centre_gate(0, GATE_F)
@@ -515,11 +495,11 @@ def tile_hyperlstmcell_pa_kernel(
         for k in range(2):
             nc.vector.tensor_copy(out=o_cols[:, k, :], in_=norm_cols[:, k * GATES + GATE_O : k * GATES + GATE_O + 1].bitcast(BF16))
         for n in range(1, BATCH_TILES):
-            prev, nxt, far = n - 1, n + 1, n + 2
+            prev, nxt = n - 1, n + 1
             mx_product(n, 0)
             if live(nxt):
-                transpose_u(nxt)
                 hh_bank = transpose_hh(nxt)
+                transpose_u(nxt)
             if n < len(to_spread):
                 spread_over_partitions(*to_spread[n])
             mx_product(n, 1)
@@ -534,23 +514,23 @@ def tile_hyperlstmcell_pa_kernel(
             gate_inv(prev, ALL)
             if n >= 2:
                 centre_cell(n - 2)
+            mean_of(n, LOW)
             finish(prev, GATE_F)
             finish(prev, GATE_I)
             finish(prev, GATE_G)
             o_shift(prev)
             if n < last:
                 cell_products(prev, nc.gpsimd)
+                quantise(nxt)
             join(n, 1)
             gate_std(n, HIGH if n == last else ALL)
-            mean_of(n, LOW)
             if n < last:
                 plain_product(nxt, 0)
                 plain_product(nxt, 1)
-                quantise(nxt)
-            if n == last:
+            else:
                 cell_products(2, nc.vector)
-            mean_of(n, HIGH)
             centre_gate(n, GATE_F)
+            mean_of(n, HIGH)
             centre_gate(n, GATE_I)
             if n == last:
                 cell_inv(0)
@@ -558,8 +538,8 @@ def tile_hyperlstmcell_pa_kernel(
                 gate_inv(n, LOW)
             centre_gate(n, GATE_G)
             if n < last:
-                cell_stats(prev)
-                pass
+                cell_sum(prev)
+                cell_spread(prev)
         for t in range(last):
             o_z(t)
         o_squash(0)
@@ -568,14 +548,16 @@ def tile_hyperlstmcell_pa_kernel(
         finish(last, GATE_I)
         finish(last, GATE_G)
         o_shift(last)
-        cell_stats(2)
+        cell_sum(2)
+        cell_spread(2)
         o_z(last)
         kept_product(last, nc.vector)
         o_back(0)
         cell_mean(2)
         cell_finish(0)
         written_product(last, nc.vector)
-        cell_stats(last)
+        cell_sum(last)
+        cell_spread(last)
         cell_finish(1)
         o_squash(1)
         centre_cell(2)

@@ -316,7 +316,7 @@ def tile_hyperlstmcell_pa_kernel(
 
         def o_shift(t):
             one = slice(GATE_O, GATE_O + 1)
-            tiny(scaled_mean[t][:], neg_mean[t][:, one], inv[t][:, one])
+            nc.vector.tensor_tensor(out=scaled_mean[t][:], in0=neg_mean[t][:, one], in1=inv[t][:, one], op=ALU.mult)
 
         def o_z(t):
             one = slice(GATE_O, GATE_O + 1)
@@ -365,7 +365,7 @@ def tile_hyperlstmcell_pa_kernel(
             )
 
         def cell_mean(t):
-            tiny(c_neg_mean[t][:], c_sum[t][:], -1.0 / UNITS)
+            nc.vector.tensor_scalar_mul(out=c_neg_mean[t][:], in0=c_sum[t][:], scalar1=-1.0 / UNITS)
 
         def centre_cell(t):
             nc.vector.scalar_tensor_tensor(
@@ -462,7 +462,7 @@ def tile_hyperlstmcell_pa_kernel(
         last = BATCH_TILES - 1
 
         def mean_of(t, some):
-            tiny(neg_mean[t][:, some], sums[t][:, some], -1.0 / UNITS)
+            nc.vector.tensor_scalar_mul(out=neg_mean[t][:, some], in0=sums[t][:, some], scalar1=-1.0 / UNITS)
 
         def cell_spread(t):
             sum_of_squares(raw_c[t][:], c_sum[t][:], c_scaled_sq[t][:])
@@ -480,7 +480,6 @@ def tile_hyperlstmcell_pa_kernel(
             squash_gate(t, j)
 
         transpose_u(1)
-        spread_ones()
         spread_over_partitions(*to_spread[0])
         join(0, 1)
         gate_std(0, ALL)

@@ -130,8 +130,8 @@ def tile_hyperlstmcell_pa_kernel(
                 out=hh_sb[:, first:end, :], in_=hyper_h[first * P : end * P, :].rearrange("(t p) k -> p t k", p=P)
             )
 
-        load_whh(0)
         load_u(0)
+        load_whh(0)
         load_w_words(0)
         for quad in range(4):
             nc.sync.dma_start(
@@ -417,9 +417,9 @@ def tile_hyperlstmcell_pa_kernel(
 
         take_mx_bank(0)
         take_mx_bank(0)
-        transpose_whh(0)
-        copy_hh(0, transpose_hh(0, mx_banks[0][1]), nc.vector.tensor_copy)
         transpose_u(0)
+        transpose_whh(0)
+        copy_hh(0, transpose_hh(0, mx_banks[0][1]), nc.scalar.copy)
         for pair in range(PASSES // 2):
             some = slice(pair * 2 * P, (pair + 1) * 2 * P)
             nc.vector.quantize_mx(

@@ -79,7 +79,7 @@ def tile_hyperlstmcell_pa_kernel(
             ]
 
         bias_row = keep.tile([P, N], BF16)
-        nc.gpsimd.memset(bias_row[:].bitcast(I32), 0)
+        nc.vector.memset(bias_row[:].bitcast(I32), 0)
         w_scales = keep.tile([P, PASSES, N], U8, align_bytes=64)
         nc.vector.memset(w_scales[:].bitcast(I32), 0)
         ident_f32 = keep.tile([P, P], F32)
@@ -96,7 +96,7 @@ def tile_hyperlstmcell_pa_kernel(
 
         hh_sb = keep.tile([P, BATCH_TILES, UNITS], BF16)
         nc.scalar.dma_start(out=hh_sb[:, 0, :], in_=hyper_h[batch_rows(0), :])
-        nc.scalar.dma_start(out=bias_row[0:1, :], in_=hc_bih.unsqueeze(0))
+        nc.gpsimd.dma_start(out=bias_row[0:1, :], in_=hc_bih.unsqueeze(0))
         warm = keep.tile([P, 1], F32)
         nc.scalar.activation(out=warm[:], in_=gate_shift[:, 0:1], func=ACT.Sigmoid)
 
@@ -130,24 +130,31 @@ def tile_hyperlstmcell_pa_kernel(
                 out=hh_sb[:, first:end, :], in_=hyper_h[first * P : end * P, :].rearrange("(t p) k -> p t k", p=P)
             )
 
-        load_u(0)
-        load_whh(0)
-        load_w_words(0)
-        for quad in range(4):
+        def load_scales(quad):
             nc.sync.dma_start(
                 out=w_scales[32 * quad : 32 * quad + 4, :, :].bitcast(I32),
                 in_=hc_Wih_scales[:, 4 * quad : 4 * quad + 4, :].bitcast(I32).rearrange("g r c -> r g c"),
             )
+
+        def load_whh_all():
+            nc.sync.dma_start(out=whh_sb[:], in_=hc_Whh.rearrange("(c p) k -> p c k", p=P))
+
+        load_whh(0)
+        nc.sync.dma_start(out=u_sb[0][:, 0:IN], in_=x[batch_rows(0), :])
+        nc.sync.dma_start(out=u_sb[0][:, IN:K], in_=h[batch_rows(0), :])
         load_whh(1)
+        load_w_words(0)
+        for quad in range(4):
+            load_scales(quad)
         load_w_words(1)
+        load_hh(1, BATCH_TILES)
+        load_u(1)
         nc.sync.dma_start(out=norm_rows[0:GATES, :], in_=hc_ln_gamma)
         nc.sync.dma_start(out=norm_rows[GATES : 2 * GATES, :], in_=hc_ln_beta)
         nc.sync.dma_start(out=norm_rows[2 * GATES : 2 * GATES + 1, :], in_=hc_lnc_gamma.unsqueeze(0))
         nc.sync.dma_start(out=norm_rows[2 * GATES + 1 : 2 * GATES + 2, :], in_=hc_lnc_beta.unsqueeze(0))
-        load_hh(1, BATCH_TILES)
-        load_u(1)
-        for t in range(2, BATCH_TILES):
-            load_u(t)
+        load_u(2)
+        load_u(3)
         nc.sync.dma_start(out=hc_sb[:], in_=hyper_c.rearrange("(t p) k -> p t k", p=P))
 
         whhT = keep.tile([P, N, K_PLAIN], BF16)
@@ -202,6 +209,12 @@ def tile_hyperlstmcell_pa_kernel(
             u_words = u_sb[t][:].bitcast(F32)
             grouped_words = grouped[t][:].bitcast(F32)
             for pair in range(PASSES // 2):
+                transpose_u_pair(t, pair)
+
+        def transpose_u_pair(t, pair):
+            u_words = u_sb[t][:].bitcast(F32)
+            grouped_words = grouped[t][:].bitcast(F32)
+            if True:
                 planes = work_psum.tile([P, 2, 2, P], F32, tag="work")
                 for gg in range(2):
                     g = 2 * pair + gg
@@ -266,6 +279,13 @@ def tile_hyperlstmcell_pa_kernel(
                 join_gate(t, j)
 
         def join_gate(t, j):
+            join_only(t, j)
+            square_gate(t, j)
+
+        def square_gate(t, j):
+            sum_of_squares(v[t][:, gate_cols(j)], sums[t][:, j : j + 1], scaled_sq[t][:, j : j + 1])
+
+        def join_only(t, j):
                 half_n = j // GATES_PER_BANK
                 nc.vector.scalar_tensor_tensor(
                     out=v[t][:, gate_cols(j)],
@@ -276,7 +296,6 @@ def tile_hyperlstmcell_pa_kernel(
                     op1=ALU.add,
                     accum_out=sums[t][:, j : j + 1],
                 )
-                sum_of_squares(v[t][:, gate_cols(j)], sums[t][:, j : j + 1], scaled_sq[t][:, j : j + 1])
 
         def gate_mean(t):
             nc.vector.tensor_scalar_mul(out=neg_mean[t][:], in0=sums[t][:], scalar1=-1.0 / UNITS)
@@ -417,9 +436,10 @@ def tile_hyperlstmcell_pa_kernel(
 
         take_mx_bank(0)
         take_mx_bank(0)
-        transpose_u(0)
         transpose_whh(0)
         copy_hh(0, transpose_hh(0, mx_banks[0][1]), nc.scalar.copy)
+        transpose_u_pair(0, 0)
+        transpose_u_pair(0, 1)
         for pair in range(PASSES // 2):
             some = slice(pair * 2 * P, (pair + 1) * 2 * P)
             nc.vector.quantize_mx(
@@ -464,8 +484,10 @@ def tile_hyperlstmcell_pa_kernel(
         def mean_of(t, some):
             nc.vector.tensor_scalar_mul(out=neg_mean[t][:, some], in0=sums[t][:, some], scalar1=-1.0 / UNITS)
 
-        def cell_spread(t):
+        def square_cell(t):
             sum_of_squares(raw_c[t][:], c_sum[t][:], c_scaled_sq[t][:])
+
+        def cell_std(t):
             std_plus_eps(c_scaled_sq[t][:], c_root[t][:], c_std[t][:])
 
         def cell_inv(t):
@@ -478,6 +500,24 @@ def tile_hyperlstmcell_pa_kernel(
         def finish(t, j):
             norm_gate(t, j)
             squash_gate(t, j)
+
+        def mx_gate(t, j):
+            half_n = j // GATES_PER_BANK
+            if len(mx_banks[t]) == half_n:
+                take_mx_bank(t)
+            for first in range(j * UNITS, (j + 1) * UNITS, P):
+                cols = slice(first - half_n * BANK, first - half_n * BANK + P)
+                for g in range(PASSES):
+                    rows = slice(g * P, (g + 1) * P)
+                    nc.tensor.matmul_mx(
+                        out=mx_banks[t][half_n][:, cols],
+                        lhsT=u_codes[t][:, rows].bitcast(FP8X4),
+                        lhsT_scale=u_scales[t][:, rows],
+                        rhs=w_words[half_n][:, g, 2 * cols.start : 2 * cols.stop].bitcast(FP4X4),
+                        rhs_scale=w_scales[:, g, first : first + P],
+                        start=(g == 0),
+                        stop=(g == PASSES - 1),
+                    )
 
         transpose_u(1)
         spread_over_partitions(*to_spread[0])
@@ -493,81 +533,109 @@ def tile_hyperlstmcell_pa_kernel(
         centre_gate(0, GATE_G)
         for k in range(2):
             nc.vector.tensor_copy(out=o_cols[:, k, :], in_=norm_cols[:, k * GATES + GATE_O : k * GATES + GATE_O + 1].bitcast(BF16))
-        for n in range(1, BATCH_TILES):
+        for n in range(1, last):
             prev, nxt = n - 1, n + 1
             mx_product(n, 0)
-            if live(nxt):
-                hh_bank = transpose_hh(nxt)
-                transpose_u(nxt)
-            if n < len(to_spread):
-                spread_over_partitions(*to_spread[n])
+            hh_bank = transpose_hh(nxt)
+            transpose_u(nxt)
+            if n == 1:
+                spread_over_partitions(*to_spread[1])
+            if n == 2:
+                spread_over_partitions(*to_spread[2])
             mx_product(n, 1)
             join_gate(n, GATE_I)
-            if n >= 2:
-                cell_mean(n - 2)
+            if n == 2:
+                cell_mean(0)
             join_gate(n, GATE_F)
-            if n == last:
-                gate_std(n, LOW)
-            else:
-                copy_hh(nxt, hh_bank, nc.vector.tensor_copy)
+            copy_hh(nxt, hh_bank, nc.vector.tensor_copy)
             gate_inv(prev, ALL)
-            if n >= 2:
-                centre_cell(n - 2)
+            if n == 2:
+                centre_cell(0)
             mean_of(n, LOW)
             finish(prev, GATE_F)
             finish(prev, GATE_I)
             finish(prev, GATE_G)
             o_shift(prev)
-            if n < last:
-                cell_products(prev, nc.gpsimd)
-                quantise(nxt)
+            cell_products(prev, nc.gpsimd)
+            quantise(nxt)
             join(n, 1)
-            gate_std(n, HIGH if n == last else ALL)
-            if n < last:
-                plain_product(nxt, 0)
-                plain_product(nxt, 1)
-            else:
-                cell_products(2, nc.vector)
+            gate_std(n, ALL)
+            plain_product(nxt, 0)
+            plain_product(nxt, 1)
             centre_gate(n, GATE_F)
             mean_of(n, HIGH)
             centre_gate(n, GATE_I)
-            if n == last:
+            if n == 2:
                 cell_inv(0)
-                cell_inv(1)
-                gate_inv(n, LOW)
             centre_gate(n, GATE_G)
-            if n < last:
-                cell_sum(prev)
-                cell_spread(prev)
-        for t in range(last):
-            o_z(t)
+            if n == 2:
+                cell_finish(0)
+            cell_sum(prev)
+            square_cell(prev)
+            if n == 1:
+                cell_std(0)
+        mx_product(last, 0)
+        mx_gate(last, GATE_G)
+        mx_gate(last, GATE_O)
+        I, F, G, O = GATE_I, GATE_F, GATE_G, GATE_O
+        just_g, just_o = slice(G, G + 1), slice(O, O + 1)
+        join_gate(last, I)
+        join_gate(last, F)
+        gate_std(last, LOW)
+        cell_mean(1)
+        join_gate(last, G)
+        gate_std(last, just_g)
+        mean_of(last, LOW)
+        gate_inv(2, ALL)
+        join_only(last, O)
+        o_z(0)
+        o_z(1)
+        finish(2, F)
+        finish(2, I)
+        mean_of(last, HIGH)
+        centre_gate(last, F)
+        square_gate(last, O)
+        gate_std(last, just_o)
+        cell_std(1)
+        finish(2, G)
         o_squash(0)
-        finish(last, GATE_F)
-        gate_inv(last, HIGH)
-        finish(last, GATE_I)
-        finish(last, GATE_G)
-        o_shift(last)
-        cell_sum(2)
-        cell_spread(2)
-        o_z(last)
-        kept_product(last, nc.vector)
+        centre_gate(last, I)
+        gate_inv(last, LOW)
+        centre_gate(last, G)
+        finish(last, F)
+        kept_product(2, nc.vector)
+        finish(last, I)
+        gate_inv(last, just_g)
+        written_product(2, nc.vector)
+        finish(last, G)
         o_back(0)
+        o_shift(2)
+        o_z(2)
+        cell_sum(2)
+        square_cell(2)
+        cell_std(2)
+        kept_product(last, nc.vector)
         cell_mean(2)
-        cell_finish(0)
+        gate_inv(last, just_o)
         written_product(last, nc.vector)
+        o_shift(last)
+        o_z(last)
+        centre_cell(1)
         cell_sum(last)
-        cell_spread(last)
-        cell_finish(1)
+        square_cell(last)
+        cell_std(last)
         o_squash(1)
+        cell_inv(1)
         centre_cell(2)
-        cell_inv(2)
         cell_mean(last)
+        cell_finish(1)
+        cell_inv(2)
         hidden_o(0)
         cell_finish(2)
         centre_cell(last)
+        cell_inv(last)
         o_back(1)
         hidden_o(1)
-        cell_inv(last)
         cell_finish(last)
         hidden_o(2)
         hidden_o(last)

@@ -79,7 +79,7 @@ def tile_hyperlstmcell_pa_kernel(
             ]
 
         bias_row = keep.tile([P, N], BF16)
-        nc.vector.memset(bias_row[:].bitcast(I32), 0)
+        nc.gpsimd.memset(bias_row[:].bitcast(I32), 0)
         w_scales = keep.tile([P, PASSES, N], U8, align_bytes=64)
         nc.vector.memset(w_scales[:].bitcast(I32), 0)
         ident_f32 = keep.tile([P, P], F32)
@@ -96,7 +96,7 @@ def tile_hyperlstmcell_pa_kernel(
 
         hh_sb = keep.tile([P, BATCH_TILES, UNITS], BF16)
         nc.scalar.dma_start(out=hh_sb[:, 0, :], in_=hyper_h[batch_rows(0), :])
-        nc.gpsimd.dma_start(out=bias_row[0:1, :], in_=hc_bih.unsqueeze(0))
+        nc.scalar.dma_start(out=bias_row[0:1, :], in_=hc_bih.unsqueeze(0))
         warm = keep.tile([P, 1], F32)
         nc.scalar.activation(out=warm[:], in_=gate_shift[:, 0:1], func=ACT.Sigmoid)
 
@@ -139,20 +139,20 @@ def tile_hyperlstmcell_pa_kernel(
         def load_whh_all():
             nc.sync.dma_start(out=whh_sb[:], in_=hc_Whh.rearrange("(c p) k -> p c k", p=P))
 
-        load_whh(0)
         nc.sync.dma_start(out=u_sb[0][:, 0:IN], in_=x[batch_rows(0), :])
         nc.sync.dma_start(out=u_sb[0][:, IN:K], in_=h[batch_rows(0), :])
-        load_whh(1)
+        load_whh(0)
         load_w_words(0)
         for quad in range(4):
             load_scales(quad)
+        load_whh(1)
         load_w_words(1)
-        load_hh(1, BATCH_TILES)
-        load_u(1)
         nc.sync.dma_start(out=norm_rows[0:GATES, :], in_=hc_ln_gamma)
         nc.sync.dma_start(out=norm_rows[GATES : 2 * GATES, :], in_=hc_ln_beta)
         nc.sync.dma_start(out=norm_rows[2 * GATES : 2 * GATES + 1, :], in_=hc_lnc_gamma.unsqueeze(0))
         nc.sync.dma_start(out=norm_rows[2 * GATES + 1 : 2 * GATES + 2, :], in_=hc_lnc_beta.unsqueeze(0))
+        load_hh(1, BATCH_TILES)
+        load_u(1)
         load_u(2)
         load_u(3)
         nc.sync.dma_start(out=hc_sb[:], in_=hyper_c.rearrange("(t p) k -> p t k", p=P))
@@ -436,10 +436,10 @@ def tile_hyperlstmcell_pa_kernel(
 
         take_mx_bank(0)
         take_mx_bank(0)
-        transpose_whh(0)
-        copy_hh(0, transpose_hh(0, mx_banks[0][1]), nc.scalar.copy)
         transpose_u_pair(0, 0)
         transpose_u_pair(0, 1)
+        transpose_whh(0)
+        copy_hh(0, transpose_hh(0, mx_banks[0][1]), nc.scalar.copy)
         for pair in range(PASSES // 2):
             some = slice(pair * 2 * P, (pair + 1) * 2 * P)
             nc.vector.quantize_mx(

@@ -501,24 +501,6 @@ def tile_hyperlstmcell_pa_kernel(
             norm_gate(t, j)
             squash_gate(t, j)
 
-        def mx_gate(t, j):
-            half_n = j // GATES_PER_BANK
-            if len(mx_banks[t]) == half_n:
-                take_mx_bank(t)
-            for first in range(j * UNITS, (j + 1) * UNITS, P):
-                cols = slice(first - half_n * BANK, first - half_n * BANK + P)
-                for g in range(PASSES):
-                    rows = slice(g * P, (g + 1) * P)
-                    nc.tensor.matmul_mx(
-                        out=mx_banks[t][half_n][:, cols],
-                        lhsT=u_codes[t][:, rows].bitcast(FP8X4),
-                        lhsT_scale=u_scales[t][:, rows],
-                        rhs=w_words[half_n][:, g, 2 * cols.start : 2 * cols.stop].bitcast(FP4X4),
-                        rhs_scale=w_scales[:, g, first : first + P],
-                        start=(g == 0),
-                        stop=(g == PASSES - 1),
-                    )
-
         transpose_u(1)
         spread_over_partitions(*to_spread[0])
         join(0, 1)
@@ -575,8 +557,7 @@ def tile_hyperlstmcell_pa_kernel(
             if n == 1:
                 cell_std(0)
         mx_product(last, 0)
-        mx_gate(last, GATE_G)
-        mx_gate(last, GATE_O)
+        mx_product(last, 1)
         I, F, G, O = GATE_I, GATE_F, GATE_G, GATE_O
         just_g, just_o = slice(G, G + 1), slice(O, O + 1)
         join_gate(last, I)
@@ -584,19 +565,17 @@ def tile_hyperlstmcell_pa_kernel(
         gate_std(last, LOW)
         cell_mean(1)
         join_gate(last, G)
-        gate_std(last, just_g)
         mean_of(last, LOW)
         gate_inv(2, ALL)
-        join_only(last, O)
+        join_gate(last, O)
+        gate_std(last, HIGH)
+        cell_std(1)
         o_z(0)
         o_z(1)
         finish(2, F)
         finish(2, I)
         mean_of(last, HIGH)
         centre_gate(last, F)
-        square_gate(last, O)
-        gate_std(last, just_o)
-        cell_std(1)
         finish(2, G)
         o_squash(0)
         centre_gate(last, I)
@@ -605,7 +584,7 @@ def tile_hyperlstmcell_pa_kernel(
         finish(last, F)
         kept_product(2, nc.vector)
         finish(last, I)
-        gate_inv(last, just_g)
+        gate_inv(last, HIGH)
         written_product(2, nc.vector)
         finish(last, G)
         o_back(0)
@@ -616,7 +595,6 @@ def tile_hyperlstmcell_pa_kernel(
         cell_std(2)
         kept_product(last, nc.vector)
         cell_mean(2)
-        gate_inv(last, just_o)
         written_product(last, nc.vector)
         o_shift(last)
         o_z(last)

@@ -140,19 +140,21 @@ def tile_hyperlstmcell_pa_kernel(
             nc.sync.dma_start(out=whh_sb[:], in_=hc_Whh.rearrange("(c p) k -> p c k", p=P))
 
         nc.sync.dma_start(out=u_sb[0][:, 0:IN], in_=x[batch_rows(0), :])
-        nc.sync.dma_start(out=u_sb[0][:, IN:K], in_=h[batch_rows(0), :])
         load_whh(0)
+        nc.sync.dma_start(out=u_sb[0][:, IN:K], in_=h[batch_rows(0), :])
         load_w_words(0)
-        for quad in range(4):
+        for quad in range(2):
             load_scales(quad)
         load_whh(1)
+        for quad in range(2, 4):
+            load_scales(quad)
         load_w_words(1)
+        load_hh(1, BATCH_TILES)
+        load_u(1)
         nc.sync.dma_start(out=norm_rows[0:GATES, :], in_=hc_ln_gamma)
         nc.sync.dma_start(out=norm_rows[GATES : 2 * GATES, :], in_=hc_ln_beta)
         nc.sync.dma_start(out=norm_rows[2 * GATES : 2 * GATES + 1, :], in_=hc_lnc_gamma.unsqueeze(0))
         nc.sync.dma_start(out=norm_rows[2 * GATES + 1 : 2 * GATES + 2, :], in_=hc_lnc_beta.unsqueeze(0))
-        load_hh(1, BATCH_TILES)
-        load_u(1)
         load_u(2)
         load_u(3)
         nc.sync.dma_start(out=hc_sb[:], in_=hyper_c.rearrange("(t p) k -> p t k", p=P))
@@ -437,9 +439,9 @@ def tile_hyperlstmcell_pa_kernel(
         take_mx_bank(0)
         take_mx_bank(0)
         transpose_u_pair(0, 0)
-        transpose_u_pair(0, 1)
         transpose_whh(0)
-        copy_hh(0, transpose_hh(0, mx_banks[0][1]), nc.scalar.copy)
+        copy_hh(0, transpose_hh(0, mx_banks[0][1]), nc.vector.tensor_copy)
+        transpose_u_pair(0, 1)
         for pair in range(PASSES // 2):
             some = slice(pair * 2 * P, (pair + 1) * 2 * P)
             nc.vector.quantize_mx(

from contextlib import ExitStack
import math

import concourse.mybir as mybir
from concourse.masks import make_identity

F32 = mybir.dt.float32
BF16 = mybir.dt.bfloat16
I32 = mybir.dt.int32
U32 = mybir.dt.uint32
U8 = mybir.dt.uint8
FP8X4 = mybir.dt.float8_e4m3fn_x4
FP4X4 = mybir.dt.float4_e2m1fn_x4
ALU = mybir.AluOpType
ACT = mybir.ActivationFunctionType

P = 128
BATCH, IN, HID, UNITS, GATES = 512, 1024, 1024, 256, 4
K = IN + HID
N = GATES * UNITS
K_PASS = 4 * P
PASSES = K // K_PASS
BANK = 512
HALVES = N // BANK
GATES_PER_BANK = BANK // UNITS
BATCH_TILES = BATCH // P
K_PLAIN = UNITS // P
RUN = 4
EPS = 1e-6
ROOT_TO_STD = 1.0 / (UNITS * math.sqrt(UNITS - 1))
GATE_I, GATE_F, GATE_G, GATE_O = 0, 1, 2, 3
CELL_GATES = (GATE_I, GATE_F, GATE_G)
GATE_FUNC = (ACT.Sigmoid, ACT.Sigmoid, ACT.Tanh, ACT.Sigmoid)

FLOPS = 2 * BATCH * K * N + 2 * BATCH * UNITS * N


def gate_cols(j):
    return slice(j * UNITS, (j + 1) * UNITS)


def batch_rows(t):
    return slice(t * P, (t + 1) * P)


def live(t):
    return 0 <= t < BATCH_TILES


def tile_hyperlstmcell_pa_kernel(
    tc,
    x,
    h,
    hyper_h,
    hyper_c,
    hc_Wih_words,
    hc_Wih_scales,
    hc_bih,
    hc_Whh,
    hc_ln_gamma,
    hc_ln_beta,
    hc_lnc_gamma,
    hc_lnc_beta,
    out_0,
    out_1,
):
    nc = tc.nc
    with ExitStack() as ctx:
        keep = ctx.enter_context(tc.tile_pool(name="keep", bufs=1))
        scrap = ctx.enter_context(tc.tile_pool(name="scrap", bufs=2))
        const_psum = ctx.enter_context(tc.psum_pool(name="const_psum", bufs=1))
        work_psum = ctx.enter_context(tc.psum_pool(name="work_psum", bufs=3))
        mx_psum = ctx.enter_context(tc.psum_pool(name="mx_psum", bufs=2))
        ctx.enter_context(tc.manual_schedule())

        def per_tile(name, shape, dtype, align_bytes=32):
            return [
                keep.tile(shape, dtype, name="%s%d" % (name, t), align_bytes=align_bytes) for t in range(BATCH_TILES)
            ]

        bias_row = keep.tile([P, N], BF16)
        nc.gpsimd.memset(bias_row[:].bitcast(I32), 0)
        w_scales = keep.tile([P, PASSES, N], U8, align_bytes=64)
        nc.vector.memset(w_scales[:].bitcast(I32), 0)
        ident_f32 = keep.tile([P, P], F32)
        make_identity(nc, ident_f32[:])
        gate_shift = keep.tile([P, GATES], F32)
        nc.vector.memset(gate_shift[:], 0.0)
        nc.vector.memset(gate_shift[:, GATE_F : GATE_F + 1], 1.0)
        norm_rows = keep.tile([P, UNITS], BF16)
        nc.vector.memset(norm_rows[:].bitcast(I32), 0)
        ones = keep.tile([P, P], BF16)
        nc.vector.memset(ones[:], 1.0)
        half = keep.tile([P, GATES], F32)
        nc.vector.memset(half[:], 0.5)

        hh_sb = keep.tile([P, BATCH_TILES, UNITS], BF16)
        nc.scalar.dma_start(out=hh_sb[:, 0, :], in_=hyper_h[batch_rows(0), :])
        nc.scalar.dma_start(out=bias_row[0:1, :], in_=hc_bih.unsqueeze(0))
        warm = keep.tile([P, 1], F32)
        nc.scalar.activation(out=warm[:], in_=gate_shift[:, 0:1], func=ACT.Sigmoid)

        u_sb = per_tile("u_sb", [P, K], BF16)
        hc_sb = keep.tile([P, BATCH_TILES, UNITS], BF16)
        whh_sb = keep.tile([P, N // P, UNITS], BF16)
        w_words = [
            keep.tile([P, PASSES, 2 * BANK], U8, name="w_words%d" % half_n, align_bytes=64) for half_n in range(HALVES)
        ]

        def load_u(t):
            nc.sync.dma_start(out=u_sb[t][:, 0:IN], in_=x[batch_rows(t), :])
            nc.sync.dma_start(out=u_sb[t][:, IN:K], in_=h[batch_rows(t), :])

        def load_whh(half_n):
            chunks = slice(half_n * BANK // P, (half_n + 1) * BANK // P)
            nc.sync.dma_start(
                out=whh_sb[:, chunks, :],
                in_=hc_Whh[half_n * BANK : (half_n + 1) * BANK, :].rearrange("(c p) k -> p c k", p=P),
            )

        def load_w_words(half_n):
            some = slice(2 * half_n * BANK, 2 * (half_n + 1) * BANK)
            nc.sync.dma_start(
                out=w_words[half_n][:].bitcast(I32),
                in_=hc_Wih_words[:, :, some].bitcast(I32).rearrange("g p c -> p g c"),
            )

        def load_hh(first, end):
            nc.sync.dma_start(
                out=hh_sb[:, first:end, :], in_=hyper_h[first * P : end * P, :].rearrange("(t p) k -> p t k", p=P)
            )

        def load_scales(quad):
            nc.sync.dma_start(
                out=w_scales[32 * quad : 32 * quad + 4, :, :].bitcast(I32),
                in_=hc_Wih_scales[:, 4 * quad : 4 * quad + 4, :].bitcast(I32).rearrange("g r c -> r g c"),
            )

        def load_whh_all():
            nc.sync.dma_start(out=whh_sb[:], in_=hc_Whh.rearrange("(c p) k -> p c k", p=P))

        nc.sync.dma_start(out=u_sb[0][:, 0:IN], in_=x[batch_rows(0), :])
        load_whh(0)
        nc.sync.dma_start(out=u_sb[0][:, IN:K], in_=h[batch_rows(0), :])
        load_w_words(0)
        for quad in range(2):
            load_scales(quad)
        load_whh(1)
        for quad in range(2, 4):
            load_scales(quad)
        load_w_words(1)
        load_hh(1, BATCH_TILES)
        load_u(1)
        nc.sync.dma_start(out=norm_rows[0:GATES, :], in_=hc_ln_gamma)
        nc.sync.dma_start(out=norm_rows[GATES : 2 * GATES, :], in_=hc_ln_beta)
        nc.sync.dma_start(out=norm_rows[2 * GATES : 2 * GATES + 1, :], in_=hc_lnc_gamma.unsqueeze(0))
        nc.sync.dma_start(out=norm_rows[2 * GATES + 1 : 2 * GATES + 2, :], in_=hc_lnc_beta.unsqueeze(0))
        load_u(2)
        load_u(3)
        nc.sync.dma_start(out=hc_sb[:], in_=hyper_c.rearrange("(t p) k -> p t k", p=P))

        whhT = keep.tile([P, N, K_PLAIN], BF16)
        gamma_bc = const_psum.tile([P, N], BF16)
        beta_bc = const_psum.tile([P, N], BF16)
        c_norm_bc = const_psum.tile([P, 2 * UNITS], BF16)
        o_cols = keep.tile([P, 2, 2], F32)
        scaled_mean = per_tile("scaled_mean", [P, 1], F32)
        z_o = per_tile("z_o", [P, 2, P], F32)
        o_units = [keep.tile([P, 2, 2, P], F32, name="o_units%d" % k) for k in range(2)]
        o_banks = [None, None]
        hhT = per_tile("hhT", [P, P, K_PLAIN], BF16)
        grouped = per_tile("grouped", [P, PASSES, P, 4], BF16, align_bytes=64)
        u_codes = per_tile("u_codes", [P, PASSES * P], U32, align_bytes=64)
        u_scales = per_tile("u_scales", [P, PASSES * P], U8, align_bytes=64)
        plain = per_tile("plain", [P, N], F32)
        mx_banks = [[] for t in range(BATCH_TILES)]
        v = per_tile("v", [P, N], F32)
        sums = per_tile("sums", [P, GATES], F32)
        scaled_sq = per_tile("scaled_sq", [P, GATES], F32)
        root = per_tile("root", [P, GATES], F32)
        std = per_tile("std", [P, GATES], F32)
        inv = per_tile("inv", [P, GATES], F32)
        neg_mean = per_tile("neg_mean", [P, GATES], F32)
        centred = per_tile("centred", [P, N], F32)
        normed = per_tile("normed", [P, N], F32)
        act = per_tile("act", [P, N], F32)
        kept = per_tile("kept", [P, UNITS], F32)
        written = per_tile("written", [P, UNITS], F32)
        raw_c = per_tile("raw_c", [P, UNITS], F32)
        c_sum = per_tile("c_sum", [P, 1], F32)
        c_scaled_sq = per_tile("c_scaled_sq", [P, 1], F32)
        c_root = per_tile("c_root", [P, 1], F32)
        c_std = per_tile("c_std", [P, 1], F32)
        c_inv = per_tile("c_inv", [P, 1], F32)
        c_neg_mean = per_tile("c_neg_mean", [P, 1], F32)
        c_centred = per_tile("c_centred", [P, UNITS], F32)
        new_c = per_tile("new_c", [P, UNITS], F32)
        tanh_c = per_tile("tanh_c", [P, UNITS], F32)
        new_h = per_tile("new_h", [P, UNITS], F32)

        def transpose_hh(t, hh_bank=None):
            if hh_bank is None:
                hh_bank = work_psum.tile([P, P], F32, tag="work")
            nc.tensor.transpose(hh_bank[:, 0:P], hh_sb[:, t, :].bitcast(F32), ident_f32[:])
            return hh_bank

        def copy_hh(t, hh_bank, engine_copy):
            engine_copy(out=hhT[t][:].rearrange("p b e -> p (b e)"), in_=hh_bank[:, 0:P].bitcast(BF16))

        def transpose_u(t):
            u_words = u_sb[t][:].bitcast(F32)
            grouped_words = grouped[t][:].bitcast(F32)
            for pair in range(PASSES // 2):
                transpose_u_pair(t, pair)

        def transpose_u_pair(t, pair):
            u_words = u_sb[t][:].bitcast(F32)
            grouped_words = grouped[t][:].bitcast(F32)
            if True:
                planes = work_psum.tile([P, 2, 2, P], F32, tag="work")
                for gg in range(2):
                    g = 2 * pair + gg
                    for w in range(2):
                        nc.tensor.transpose(
                            planes[:, gg, w, :], u_words[:, 256 * g + w : 256 * (g + 1) : 2], ident_f32[:]
                        )
                nc.scalar.copy(
                    out=grouped_words[:, 2 * pair : 2 * pair + 2, :, :],
                    in_=planes[:].rearrange("p g w b -> p g b w"),
                )

        def quantise(t):
            nc.vector.quantize_mx(
                out=u_codes[t][:].bitcast(FP8X4),
                scales=u_scales[t][:],
                in_=grouped[t][:].rearrange("p g b j -> p (g b j)"),
            )

        def plain_product(t, half_n):
            cols = slice(half_n * BANK, (half_n + 1) * BANK)
            acc = work_psum.tile([P, BANK], F32, tag="work")
            for e in range(K_PLAIN):
                nc.tensor.matmul(acc[:], lhsT=hhT[t][:, :, e], rhs=whhT[:, cols, e], start=(e == 0), stop=False)
            nc.tensor.matmul(acc[:], lhsT=ones[:], rhs=bias_row[:, cols], start=False, stop=True)
            nc.scalar.copy(out=plain[t][:, cols], in_=acc[:])

        def take_mx_bank(t):
            mx_banks[t].append(mx_psum.tile([P, BANK], F32, tag="mx", name="mx_acc"))

        def mx_product(t, half_n):
            if len(mx_banks[t]) == half_n:
                take_mx_bank(t)
            bank = mx_banks[t][half_n]
            for g in range(PASSES):
                rows = slice(g * P, (g + 1) * P)
                nc.tensor.matmul_mx(
                    out=bank[:],
                    lhsT=u_codes[t][:, rows].bitcast(FP8X4),
                    lhsT_scale=u_scales[t][:, rows],
                    rhs=w_words[half_n][:, g, :].bitcast(FP4X4),
                    rhs_scale=w_scales[:, g, half_n * BANK : (half_n + 1) * BANK],
                    start=(g == 0),
                    stop=(g == PASSES - 1),
                )

        def sum_of_squares(values, total, out):
            squares = scrap.tile([P, UNITS], F32, tag="squares")
            nc.scalar.activation(
                out=squares[:], in_=values, func=ACT.Square, scale=-float(UNITS), bias=total, accum_out=out
            )

        def std_plus_eps(sq, sq_root, out):
            width = sq.shape[1]
            nc.gpsimd.tensor_tensor(out=sq_root, in0=sq, in1=half[:, 0:width], op=ALU.pow)
            nc.gpsimd.tensor_scalar(
                out=out, in0=sq_root, scalar1=ROOT_TO_STD, scalar2=EPS, op0=ALU.mult, op1=ALU.add
            )

        def join(t, half_n):
            for j in range(half_n * GATES_PER_BANK, (half_n + 1) * GATES_PER_BANK):
                join_gate(t, j)

        def join_gate(t, j):
            join_only(t, j)
            square_gate(t, j)

        def square_gate(t, j):
            sum_of_squares(v[t][:, gate_cols(j)], sums[t][:, j : j + 1], scaled_sq[t][:, j : j + 1])

        def join_only(t, j):
                half_n = j // GATES_PER_BANK
                nc.vector.scalar_tensor_tensor(
                    out=v[t][:, gate_cols(j)],
                    in0=mx_banks[t][half_n][:, gate_cols(j % GATES_PER_BANK)],
                    scalar=1.0,
                    in1=plain[t][:, gate_cols(j)],
                    op0=ALU.mult,
                    op1=ALU.add,
                    accum_out=sums[t][:, j : j + 1],
                )

        def gate_mean(t):
            nc.vector.tensor_scalar_mul(out=neg_mean[t][:], in0=sums[t][:], scalar1=-1.0 / UNITS)

        def centre_gate(t, j):
            nc.vector.scalar_tensor_tensor(
                out=centred[t][:, gate_cols(j)],
                in0=v[t][:, gate_cols(j)],
                scalar=neg_mean[t][:, j : j + 1],
                in1=gamma_bc[:, gate_cols(j)],
                op0=ALU.add,
                op1=ALU.mult,
            )

        def norm_gate(t, j):
            nc.vector.scalar_tensor_tensor(
                out=normed[t][:, gate_cols(j)],
                in0=centred[t][:, gate_cols(j)],
                scalar=inv[t][:, j : j + 1],
                in1=beta_bc[:, gate_cols(j)],
                op0=ALU.mult,
                op1=ALU.add,
            )

        def squash_gate(t, j):
            nc.scalar.activation(
                out=act[t][:, gate_cols(j)],
                in_=normed[t][:, gate_cols(j)],
                func=GATE_FUNC[j],
                bias=gate_shift[:, j : j + 1],
            )

        unit = gamma_bc[:, gate_cols(GATE_O)]

        def tiny(out, in_, factor):
            nc.vector.scalar_tensor_tensor(out=out, in0=in_, scalar=factor, in1=unit[:, 0 : out.shape[1]], op0=ALU.mult, op1=ALU.mult)

        def o_shift(t):
            one = slice(GATE_O, GATE_O + 1)
            nc.vector.tensor_tensor(out=scaled_mean[t][:], in0=neg_mean[t][:, one], in1=inv[t][:, one], op=ALU.mult)

        def o_z(t):
            one = slice(GATE_O, GATE_O + 1)
            nc.scalar.activation(out=z_o[t][:], in_=v[t][:, gate_cols(GATE_O)].rearrange("p (q e) -> p e q", e=2), func=ACT.Identity, scale=inv[t][:, one], bias=scaled_mean[t][:])

        def o_squash(k):
            bank = work_psum.tile([P, 2, 2, P], F32, tag="work")
            for i in range(2):
                for e in range(2):
                    nc.tensor.transpose(bank[:, e, i, :], z_o[2 * k + i][:, e, :], ident_f32[:])
            for e in range(2):
                nc.scalar.activation(out=o_units[k][:, e, :, :], in_=bank[:, e, :, :], func=ACT.Sigmoid, scale=o_cols[:, 0, e : e + 1], bias=o_cols[:, 1, e : e + 1])

        def o_back(k):
            bank = work_psum.tile([P, 2, 2, P], F32, tag="work")
            for i in range(2):
                for e in range(2):
                    nc.tensor.transpose(bank[:, i, e, :], o_units[k][:, e, i, :], ident_f32[:])
            o_banks[k] = bank

        def hidden_o(t):
            nc.vector.tensor_tensor(out=new_h[t][:].rearrange("p (q e) -> p q e", e=2), in0=tanh_c[t][:].rearrange("p (q e) -> p q e", e=2), in1=o_banks[t // 2][:, t % 2, :, :].rearrange("p e q -> p q e"), op=ALU.mult)
            nc.sync.dma_start(out=out_0[batch_rows(t), :], in_=new_h[t][:])

        def kept_product(t, engine):
            engine.tensor_tensor(out=kept[t][:], in0=hc_sb[:, t, :], in1=act[t][:, gate_cols(GATE_F)], op=ALU.mult)

        def written_product(t, engine):
            engine.tensor_tensor(
                out=written[t][:], in0=act[t][:, gate_cols(GATE_I)], in1=act[t][:, gate_cols(GATE_G)], op=ALU.mult
            )

        def cell_products(t, engine):
            kept_product(t, engine)
            written_product(t, engine)

        def cell_sum(t):
            nc.vector.scalar_tensor_tensor(
                out=raw_c[t][:],
                in0=kept[t][:],
                scalar=1.0,
                in1=written[t][:],
                op0=ALU.mult,
                op1=ALU.add,
                accum_out=c_sum[t][:],
            )

        def cell_mean(t):
            nc.vector.tensor_scalar_mul(out=c_neg_mean[t][:], in0=c_sum[t][:], scalar1=-1.0 / UNITS)

        def centre_cell(t):
            nc.vector.scalar_tensor_tensor(
                out=c_centred[t][:],
                in0=raw_c[t][:],
                scalar=c_neg_mean[t][:],
                in1=c_norm_bc[:, 0:UNITS],
                op0=ALU.add,
                op1=ALU.mult,
            )

        def norm_cell(t):
            nc.vector.scalar_tensor_tensor(
                out=new_c[t][:],
                in0=c_centred[t][:],
                scalar=c_inv[t][:],
                in1=c_norm_bc[:, UNITS : 2 * UNITS],
                op0=ALU.mult,
                op1=ALU.add,
            )
            nc.sync.dma_start(out=out_1[batch_rows(t), :], in_=new_c[t][:])

        def hidden(t, engine):
            engine.tensor_tensor(out=new_h[t][:], in0=tanh_c[t][:], in1=act[t][:, gate_cols(GATE_O)], op=ALU.mult)
            nc.sync.dma_start(out=out_0[batch_rows(t), :], in_=new_h[t][:])

        whh_words = whh_sb[:].bitcast(F32)

        def transpose_whh(half_n):
            whh_bank = work_psum.tile([P, RUN, P], F32, tag="work")
            for i in range(RUN):
                nc.tensor.transpose(whh_bank[:, i, :], whh_words[:, half_n * RUN + i, :], ident_f32[:])
            nc.vector.tensor_copy(
                out=whhT[:, half_n * BANK : (half_n + 1) * BANK, :].rearrange("p n e -> p (n e)"),
                in_=whh_bank[:].rearrange("p i n -> p (i n)").bitcast(BF16),
            )

        def spread_over_partitions(first, spread):
            spread_words = spread[:].bitcast(F32)
            for c in range(min(3, spread_words.shape[1] // P)):
                nc.tensor.transpose(
                    spread_words[:, c * P : (c + 1) * P],
                    norm_cols[:, first + c : first + c + 1].to_broadcast([P, P]),
                    ident_f32[:],
                )

        def spread_ones():
            nc.tensor.transpose(gamma_bc[:].bitcast(F32)[:, 3 * P : 4 * P], ones[:].bitcast(F32)[:, 0:1].to_broadcast([P, P]), ident_f32[:])

        take_mx_bank(0)
        take_mx_bank(0)
        transpose_u_pair(0, 0)
        transpose_whh(0)
        copy_hh(0, transpose_hh(0, mx_banks[0][1]), nc.vector.tensor_copy)
        transpose_u_pair(0, 1)
        for pair in range(PASSES // 2):
            some = slice(pair * 2 * P, (pair + 1) * 2 * P)
            nc.vector.quantize_mx(
                out=u_codes[0][:, some].bitcast(FP8X4),
                scales=u_scales[0][:, some],
                in_=grouped[0][:, 2 * pair : 2 * pair + 2, :, :].rearrange("p g b j -> p (g b j)"),
            )
        plain_product(0, 0)
        transpose_whh(1)
        mx_product(0, 0)
        plain_product(0, 1)
        join(0, 0)
        mx_product(0, 1)
        norm_cols_bank = work_psum.tile([P, P], F32, tag="work")
        nc.tensor.transpose(norm_cols_bank[:], norm_rows[:].bitcast(F32), ident_f32[:])
        norm_cols = keep.tile([P, 2 * GATES + 2], F32)
        nc.vector.tensor_copy(out=norm_cols[:], in_=norm_cols_bank[:, 0 : 2 * GATES + 2])
        copy_hh(1, transpose_hh(1), nc.vector.tensor_copy)
        to_spread = [(0, gamma_bc), (GATES, beta_bc), (2 * GATES, c_norm_bc)]

        def squash_cell(t):
            nc.scalar.activation(out=tanh_c[t][:], in_=new_c[t][:], func=ACT.Tanh)

        def by_bank(t):
            return t == BATCH_TILES - 1

        def bank_gates(half_n):
            return slice(half_n * GATES_PER_BANK, (half_n + 1) * GATES_PER_BANK)

        def gate_std(t, gates):
            std_plus_eps(scaled_sq[t][:, gates], root[t][:, gates], std[t][:, gates])

        def gate_inv(t, gates):
            nc.vector.reciprocal(out=inv[t][:, gates], in_=std[t][:, gates])

        def gates(a, b):
            return slice(a, b)

        LOW, HIGH, ALL = slice(0, 2), slice(2, 4), slice(0, 4)
        last = BATCH_TILES - 1

        def mean_of(t, some):
            nc.vector.tensor_scalar_mul(out=neg_mean[t][:, some], in0=sums[t][:, some], scalar1=-1.0 / UNITS)

        def square_cell(t):
            sum_of_squares(raw_c[t][:], c_sum[t][:], c_scaled_sq[t][:])

        def cell_std(t):
            std_plus_eps(c_scaled_sq[t][:], c_root[t][:], c_std[t][:])

        def cell_inv(t):
            nc.vector.reciprocal(out=c_inv[t][:], in_=c_std[t][:])

        def cell_finish(t):
            norm_cell(t)
            squash_cell(t)

        def finish(t, j):
            norm_gate(t, j)
            squash_gate(t, j)

        transpose_u(1)
        spread_over_partitions(*to_spread[0])
        join(0, 1)
        gate_std(0, ALL)
        mean_of(0, LOW)
        plain_product(1, 0)
        plain_product(1, 1)
        centre_gate(0, GATE_F)
        quantise(1)
        mean_of(0, HIGH)
        centre_gate(0, GATE_I)
        centre_gate(0, GATE_G)
        for k in range(2):
            nc.vector.tensor_copy(out=o_cols[:, k, :], in_=norm_cols[:, k * GATES + GATE_O : k * GATES + GATE_O + 1].bitcast(BF16))
        for n in range(1, last):
            prev, nxt = n - 1, n + 1
            mx_product(n, 0)
            hh_bank = transpose_hh(nxt)
            transpose_u(nxt)
            if n == 1:
                spread_over_partitions(*to_spread[1])
            if n == 2:
                spread_over_partitions(*to_spread[2])
            mx_product(n, 1)
            join_gate(n, GATE_I)
            if n == 2:
                cell_mean(0)
            join_gate(n, GATE_F)
            copy_hh(nxt, hh_bank, nc.vector.tensor_copy)
            gate_inv(prev, ALL)
            if n == 2:
                centre_cell(0)
            mean_of(n, LOW)
            finish(prev, GATE_F)
            finish(prev, GATE_I)
            finish(prev, GATE_G)
            o_shift(prev)
            cell_products(prev, nc.gpsimd)
            quantise(nxt)
            join(n, 1)
            gate_std(n, ALL)
            plain_product(nxt, 0)
            plain_product(nxt, 1)
            centre_gate(n, GATE_F)
            mean_of(n, HIGH)
            centre_gate(n, GATE_I)
            if n == 2:
                cell_inv(0)
            centre_gate(n, GATE_G)
            if n == 2:
                cell_finish(0)
            cell_sum(prev)
            square_cell(prev)
            if n == 1:
                cell_std(0)
        mx_product(last, 0)
        mx_product(last, 1)
        I, F, G, O = GATE_I, GATE_F, GATE_G, GATE_O
        just_g, just_o = slice(G, G + 1), slice(O, O + 1)
        join_gate(last, I)
        join_gate(last, F)
        gate_std(last, LOW)
        cell_mean(1)
        join_gate(last, G)
        mean_of(last, LOW)
        gate_inv(2, ALL)
        join_gate(last, O)
        gate_std(last, HIGH)
        cell_std(1)
        o_z(0)
        o_z(1)
        finish(2, F)
        finish(2, I)
        mean_of(last, HIGH)
        centre_gate(last, F)
        finish(2, G)
        o_squash(0)
        centre_gate(last, I)
        gate_inv(last, LOW)
        centre_gate(last, G)
        finish(last, F)
        kept_product(2, nc.vector)
        finish(last, I)
        gate_inv(last, HIGH)
        written_product(2, nc.vector)
        finish(last, G)
        o_back(0)
        o_shift(2)
        o_z(2)
        cell_sum(2)
        square_cell(2)
        cell_std(2)
        kept_product(last, nc.vector)
        cell_mean(2)
        written_product(last, nc.vector)
        o_shift(last)
        o_z(last)
        centre_cell(1)
        cell_sum(last)
        square_cell(last)
        cell_std(last)
        o_squash(1)
        cell_inv(1)
        centre_cell(2)
        cell_mean(last)
        cell_finish(1)
        cell_inv(2)
        hidden_o(0)
        cell_finish(2)
        centre_cell(last)
        cell_inv(last)
        o_back(1)
        hidden_o(1)
        cell_finish(last)
        hidden_o(2)
        hidden_o(last)
